import numpy as np
import ml_dtypes


def mxq(x, axis, fmt="e4m3"):
    dtype, down = {"e4m3": (ml_dtypes.float8_e4m3fn, 7), "e5m2": (ml_dtypes.float8_e5m2, 14)}[fmt]
    v = np.moveaxis(np.asarray(x, np.float32).astype(ml_dtypes.bfloat16).astype(np.float64), axis, -1)
    blocks = v.reshape(v.shape[:-1] + (-1, 32))
    amax = np.abs(blocks).max(-1, keepdims=True)
    byte = np.maximum(np.where(amax > 0, np.frexp(amax)[1] - 1 + 127, 0) - down, 1)
    scale = np.exp2(byte - 127.0)
    codes = (blocks / scale).astype(np.float32).astype(dtype).astype(np.float64)
    return np.moveaxis((codes * scale).reshape(v.shape), -1, axis)


WIDE = False


def mx_kscale(k):
    if not WIDE:
        return np.ones(k)
    levels = np.array([10, -10, 5, -5, 0])
    a = np.random.permutation(np.resize(levels, k // 512 * 4)).reshape(k // 512, 4)
    idx = np.arange(k)
    return np.exp2(a[idx // 512, idx % 128 // 32])


BF16 = ml_dtypes.bfloat16


def bf(x):
    return np.asarray(x, np.float32).astype(BF16)


def f64(x):
    return np.asarray(x).astype(np.float64)


E2M1 = np.array([0.0, 0.5, 1.0, 1.5, 2.0, 3.0, 4.0, 6.0, -0.0, -0.5, -1.0, -1.5, -2.0, -3.0, -4.0, -6.0])


def pack_weight(w, fmt):
    k, n = w.shape
    w = f64(bf(w)).reshape(k // 32, 32, n)
    amax = np.abs(w).max(1)
    if fmt == "e4m3":
        byte = np.frexp(amax)[1] - 1 + 127 - 7
    else:
        mant, ex = np.frexp(amax / 6.0)
        byte = np.where(mant > 0.5, ex, ex - 1) + 127
    byte = np.clip(np.where(amax > 0, byte, 1), 1, 254)
    scaled = (w * np.exp2(127.0 - byte)[:, None, :]).reshape(k, n).astype(np.float32)
    by_word = np.ascontiguousarray(scaled.reshape(k // 512, 128, 4, n).transpose(0, 1, 3, 2))
    if fmt == "e4m3":
        words = by_word.astype(ml_dtypes.float8_e4m3fn).view(np.uint8)
    else:
        c = by_word.astype(ml_dtypes.float4_e2m1fn).view(np.uint8) & 0xF
        words = c[..., 0::2] | (c[..., 1::2] << 4)
    return np.ascontiguousarray(words), np.ascontiguousarray(byte.astype(np.uint8).reshape(k // 512, 16, n))


def unpack_weight(words, scales, fmt):
    g, p, n, _ = words.shape
    if fmt == "e4m3":
        vals = np.ascontiguousarray(words).view(ml_dtypes.float8_e4m3fn).astype(np.float64)
    else:
        nib = np.empty((g, p, n, 4), np.uint8)
        nib[..., 0::2] = words & 0xF
        nib[..., 1::2] = words >> 4
        vals = E2M1[nib]
    vals = vals * np.repeat(np.exp2(scales.astype(np.float64) - 127.0), 8, axis=1)[..., None]
    return vals.transpose(0, 1, 3, 2).reshape(g * 512, n)


B, S, D, H, HD = 8, 512, 512, 2, 128
E = H * HD
EPS = 1e-5
NEG = -1e9


def get_slopes(n):
    start = 2.0 ** (-2.0 ** (-(np.log2(n) - 3)))
    return np.array([start * start ** i for i in range(n)])


def prior_bias(shape, scale, loc):
    q_pos = np.arange(S, dtype=np.float64)
    k_pos = np.arange(S, dtype=np.float64)
    dist = (k_pos[None, :] - q_pos[:, None])[None, None]
    loc_t = np.exp(loc) - np.exp(-loc)
    z = (dist - loc_t) * np.exp(scale)
    return -(np.abs(z) + EPS) ** shape


def setup_inputs():
    s = mx_kscale(D)
    causal = np.tril(np.ones((S, S), dtype=bool))
    x = bf(np.random.standard_normal((B, S, D)) * s)
    wv_words, wv_scales = pack_weight(np.random.standard_normal((D, E)) * 2.0 / np.sqrt(D) / s[:, None], "e4m3")
    return {"x": x,
            "wv_words": wv_words,
            "wv_scales": wv_scales,
            "q": bf(np.random.standard_normal((B, S, H, HD))),
            "k": bf(np.random.standard_normal((B, S, H, HD))),
            "mask": bf(np.where(causal, 0.0, NEG))[None, None],
            "shape": bf(1.0 + 0.1 * np.random.standard_normal((1, H, 1, 1))),
            "scale": bf(np.log(get_slopes(H)).reshape(1, H, 1, 1) + 0.1 * np.random.standard_normal((1, H, 1, 1))),
            "loc": bf(-2.0 + 0.5 * np.random.standard_normal((1, H, 1, 1)))}


def reference(x, wv_words, wv_scales, q, k, mask, shape, scale, loc):
    v = (mxq(f64(x), 2, "e4m3") @ unpack_weight(wv_words, wv_scales, "e4m3")).reshape(B, S, H, HD)
    s = f64(q).transpose(0, 2, 1, 3) @ f64(k).transpose(0, 2, 3, 1) / np.sqrt(HD)
    s = s + prior_bias(f64(shape), f64(scale), f64(loc))
    s = s + f64(mask)
    e = np.exp(s - s.max(-1, keepdims=True))
    o = (mxq(e, 3, "e4m3") @ mxq(v.transpose(0, 2, 1, 3), 2, "e4m3")) / e.sum(-1, keepdims=True)
    return o.transpose(0, 2, 1, 3).reshape(B, S, E)

@@ -1,0 +1,250 @@
+from contextlib import ExitStack
+
+import concourse.mybir as mybir
+from concourse.masks import make_identity
+
+F32 = mybir.dt.float32
+BF16 = mybir.dt.bfloat16
+I32 = mybir.dt.int32
+U32 = mybir.dt.uint32
+U8 = mybir.dt.uint8
+FP8X4 = mybir.dt.float8_e4m3fn_x4
+ALU = mybir.AluOpType
+ACT = mybir.ActivationFunctionType
+
+B, S, D, H, HD = 8, 512, 512, 2, 128
+E = H * HD
+P = 128
+NT = S // P
+PACK = 4
+PAIRS = NT // 2
+EPS = 1e-5
+ROOT_HD = HD**0.5
+SPAN = 2 * S - P
+
+FLOPS = 2 * B * S * D * E + 2 * (2 * B * H * S * S * HD)
+
+
+def tile_bayesianattention_pa_t_kernel(tc, x, wv_words, wv_scales, q, k, mask, shape, scale, loc, out):
+    nc = tc.nc
+    with ExitStack() as ctx:
+        const = ctx.enter_context(tc.tile_pool(name="const", bufs=1))
+        inputs = ctx.enter_context(tc.tile_pool(name="inputs", bufs=B))
+        batch = ctx.enter_context(tc.tile_pool(name="batch", bufs=2))
+        work = ctx.enter_context(tc.tile_pool(name="work", bufs=3))
+        prep_psum = ctx.enter_context(tc.psum_pool(name="prep_psum", bufs=2))
+        score_psum = ctx.enter_context(tc.psum_pool(name="score_psum", bufs=2))
+        turned_psum = ctx.enter_context(tc.psum_pool(name="turned_psum", bufs=2))
+        out_psum = ctx.enter_context(tc.psum_pool(name="out_psum", bufs=2))
+
+        shape_bf = const.tile([P, H], BF16)
+        scale_bf = const.tile([P, H], BF16)
+        loc_bf = const.tile([P, H], BF16)
+        for dst, src in ((shape_bf, shape), (scale_bf, scale), (loc_bf, loc)):
+            nc.scalar.dma_start(out=dst[:], in_=src.rearrange("a h b c -> (a h b c)").partition_broadcast(P))
+
+        q_sb, k_sb, x_sb = [], [], []
+
+        def load_batch(b):
+            q_sb.append(inputs.tile([P, NT, E], BF16, name="q_sb"))
+            nc.sync.dma_start(out=q_sb[b][:], in_=q[b].rearrange("(t p) h d -> p t (h d)", p=P))
+            k_sb.append(inputs.tile([P, NT, E], BF16, name="k_sb"))
+            nc.sync.dma_start(out=k_sb[b][:], in_=k[b].rearrange("(t p) h d -> p t (h d)", p=P))
+            x_sb.append(inputs.tile([P, PACK, D], BF16, name="x_sb"))
+            nc.sync.dma_start(
+                out=x_sb[b][:].rearrange("p (u e) c -> p u (e c)", u=2),
+                in_=x[b].rearrange("(u p e) c -> p u (e c)", u=2, e=2),
+            )
+
+        load_batch(0)
+
+        w_codes = const.tile([P, E], U32, align_bytes=64)
+        w_scales = const.tile([P, E], U8, align_bytes=64)
+        nc.vector.memset(w_scales[:].bitcast(I32), 0)
+        nc.sync.dma_start(out=w_codes[:].bitcast(I32), in_=wv_words[0].rearrange("p n t -> p (n t)").bitcast(I32))
+        for quad in range(4):
+            nc.sync.dma_start(
+                out=w_scales[32 * quad : 32 * quad + 4, :].bitcast(I32),
+                in_=wv_scales[0, 4 * quad : 4 * quad + 4, :].bitcast(I32),
+            )
+        mask_sb = const.tile([P, NT, S], BF16)
+        nc.sync.dma_start(out=mask_sb[:], in_=mask[0, 0].rearrange("(t p) j -> p t j", p=P))
+        for b in range(1, B):
+            load_batch(b)
+
+        ident_f32 = const.tile([P, P], F32)
+        make_identity(nc, ident_f32[:])
+        ident_bf = const.tile([P, P], BF16)
+        make_identity(nc, ident_bf[:])
+
+        dist = const.tile([P, SPAN], I32)
+        nc.gpsimd.iota(dist[:], pattern=[[-1, SPAN]], base=S - P, channel_multiplier=1)
+        eps_col = const.tile([P, 1], F32)
+        nc.vector.memset(eps_col[:], EPS)
+        shape_f = const.tile([P, H], F32)
+        nc.vector.tensor_copy(out=shape_f[:], in_=shape_bf[:])
+        slope = const.tile([P, H], F32)
+        nc.scalar.activation(out=slope[:], in_=scale_bf[:], func=ACT.Exp)
+        exp_loc = const.tile([P, H], F32)
+        nc.scalar.activation(out=exp_loc[:], in_=loc_bf[:], func=ACT.Exp)
+        exp_neg_loc = const.tile([P, H], F32)
+        nc.scalar.activation(out=exp_neg_loc[:], in_=loc_bf[:], func=ACT.Exp, scale=-1.0)
+        offset = const.tile([P, H], F32)
+        nc.vector.tensor_sub(out=offset[:], in0=exp_loc[:], in1=exp_neg_loc[:])
+
+        z = const.tile([P, H, SPAN], F32)
+        for h in range(H):
+            nc.vector.tensor_scalar(
+                out=z[:, h, :], in0=dist[:], scalar1=offset[:, h : h + 1], scalar2=slope[:, h : h + 1],
+                op0=ALU.subtract, op1=ALU.mult,
+            )
+        nc.scalar.activation(out=z[:], in_=z[:], func=ACT.Abs)
+        nc.scalar.activation(out=z[:], in_=z[:], func=ACT.Ln, bias=eps_col[:])
+        power = const.tile([P, H, SPAN], F32)
+        for h in range(H):
+            nc.scalar.activation(out=power[:, h, :], in_=z[:, h, :], func=ACT.Exp, scale=shape_f[:, h : h + 1])
+
+        table = const.tile([P, H, NT, S], F32)
+        mask_scaled = const.tile([P, NT, S], F32)
+        for half in range(2):
+            mask_t = prep_psum.tile([P, 2, S], BF16, tag="prep")
+            for jj in range(2):
+                jt = 2 * half + jj
+                for it in range(NT):
+                    nc.tensor.transpose(
+                        mask_t[:, jj, it * P : (it + 1) * P], mask_sb[:, it, jt * P : (jt + 1) * P], ident_bf[:]
+                    )
+            nc.scalar.activation(
+                out=mask_scaled[:, 2 * half : 2 * half + 2, :], in_=mask_t[:], func=ACT.Copy, scale=ROOT_HD
+            )
+        for h in range(H):
+            for jt in range(NT):
+                first = S - P - P * jt
+                nc.vector.scalar_tensor_tensor(
+                    out=table[:, h, jt, :], in0=power[:, h, first : first + S], scalar=-ROOT_HD,
+                    in1=mask_scaled[:, jt, :], op0=ALU.mult, op1=ALU.add,
+                )
+
+        def prepare(b):
+            turned = []
+            for name, rows in (("q_t", q_sb[b]), ("k_t", k_sb[b])):
+                t_ps = prep_psum.tile([P, H, S], BF16, tag="prep")
+                for h in range(H):
+                    for t in range(NT):
+                        nc.tensor.transpose(
+                            t_ps[:, h, t * P : (t + 1) * P], rows[:, t, h * HD : (h + 1) * HD], ident_bf[:]
+                        )
+                t_sb = batch.tile([P, H, S], BF16, name=name)
+                nc.scalar.copy(out=t_sb[:], in_=t_ps[:])
+                turned.append(t_sb)
+
+            x_words = x_sb[b][:].bitcast(F32)
+            x_grouped = batch.tile([P, PACK, P, PACK], BF16, align_bytes=64)
+            x_grouped_words = (
+                x_grouped[:].rearrange("p t r c -> p (t r c)").bitcast(F32).rearrange("p (t r f) -> p t r f", t=PACK, f=2)
+            )
+            for half in range(2):
+                x_ps = prep_psum.tile([P, 2, 2, P], F32, tag="prep")
+                for tt in range(2):
+                    for f in range(2):
+                        nc.tensor.transpose(x_ps[:, tt, f, :], x_words[:, 2 * half + tt, f : D // 2 : 2], ident_f32[:])
+                nc.vector.tensor_copy(
+                    out=x_grouped_words[:, 2 * half : 2 * half + 2, :, :], in_=x_ps[:].rearrange("p t f r -> p t r f")
+                )
+            x_codes = batch.tile([P, PACK * P], U32, align_bytes=64)
+            x_scales = batch.tile([P, PACK * P], U8, align_bytes=64)
+            nc.vector.quantize_mx(
+                out=x_codes[:].bitcast(FP8X4), scales=x_scales[:], in_=x_grouped[:].rearrange("p t r c -> p (t r c)")
+            )
+
+            v_grouped = batch.tile([P, H, HD, PACK], BF16, align_bytes=64)
+            for h in range(H):
+                v_ps = prep_psum.tile([P, PACK, HD], F32, tag="prep")
+                for t in range(PACK):
+                    nc.tensor.matmul_mx(
+                        out=v_ps[:, t, :],
+                        lhsT=x_codes[:, t * P : (t + 1) * P].bitcast(FP8X4),
+                        lhsT_scale=x_scales[:, t * P : (t + 1) * P],
+                        rhs=w_codes[:, h * HD : (h + 1) * HD].bitcast(FP8X4),
+                        rhs_scale=w_scales[:, h * HD : (h + 1) * HD],
+                        start=True,
+                        stop=True,
+                    )
+                nc.scalar.copy(out=v_grouped[:, h, :, :], in_=v_ps[:].rearrange("p t d -> p d t"))
+            v_codes = batch.tile([P, E], U32, align_bytes=64)
+            v_scales = batch.tile([P, E], U8, align_bytes=64)
+            nc.vector.quantize_mx(
+                out=v_codes[:].bitcast(FP8X4), scales=v_scales[:], in_=v_grouped[:].rearrange("p h d t -> p (h d t)")
+            )
+            return turned[0], turned[1], v_codes, v_scales
+
+        def attend(b, pair, ready):
+            q_t, k_t, v_codes, v_scales = ready
+            neg_max = work.tile([P, 2, H], F32)
+            row_sum = work.tile([P, 2, H], F32)
+            o_ps = out_psum.tile([P, 2, H, HD], F32)
+            for h in range(H):
+                e_ps = turned_psum.tile([P, 2, 2, P], F32)
+                for ii in range(2):
+                    it = 2 * pair + ii
+                    s_ps = score_psum.tile([P, S], F32)
+                    nc.tensor.matmul(
+                        out=s_ps[:], lhsT=q_t[:, h, it * P : (it + 1) * P], rhs=k_t[:, h, :], start=True, stop=False
+                    )
+                    for jt in range(NT):
+                        nc.tensor.matmul(
+                            out=s_ps[:, jt * P : (jt + 1) * P],
+                            lhsT=table[:, h, jt, it * P : (it + 1) * P],
+                            rhs=ident_f32[:],
+                            is_transpose=True,
+                            start=False,
+                            stop=(jt == NT - 1),
+                        )
+                    neg_s = work.tile([P, S], F32)
+                    nc.vector.tensor_scalar(
+                        out=neg_s[:], in0=s_ps[:], scalar1=-1.0 / ROOT_HD, scalar2=None,
+                        op0=ALU.mult, op1=ALU.min, accum_out=neg_max[:, ii, h : h + 1],
+                    )
+                    e_sb = work.tile([P, S], BF16)
+                    nc.scalar.activation(
+                        out=e_sb[:], in_=neg_s[:], func=ACT.Exp, scale=-1.0, bias=neg_max[:, ii, h : h + 1],
+                        accum_out=row_sum[:, ii, h : h + 1],
+                    )
+                    e_words = e_sb[:].bitcast(F32)
+                    for u in range(2):
+                        nc.tensor.transpose(e_ps[:, ii, u, :], e_words[:, u * P : (u + 1) * P], ident_f32[:])
+                e_grouped = work.tile([P, 2, P, PACK], BF16, align_bytes=64)
+                nc.scalar.copy(
+                    out=e_grouped[:].rearrange("p t i c -> p (t i c)").bitcast(F32).rearrange("p (t i u) -> p t i u", t=2, u=2),
+                    in_=e_ps[:].rearrange("p t u i -> p t i u"),
+                )
+                e_codes = work.tile([P, 2 * P], U32, align_bytes=64)
+                e_scales = work.tile([P, 2 * P], U8, align_bytes=64)
+                nc.vector.quantize_mx(
+                    out=e_codes[:].bitcast(FP8X4), scales=e_scales[:], in_=e_grouped[:].rearrange("p t i c -> p (t i c)")
+                )
+                for ii in range(2):
+                    nc.tensor.matmul_mx(
+                        out=o_ps[:, ii, h, :],
+                        lhsT=e_codes[:, ii * P : (ii + 1) * P].bitcast(FP8X4),
+                        lhsT_scale=e_scales[:, ii * P : (ii + 1) * P],
+                        rhs=v_codes[:, h * HD : (h + 1) * HD].bitcast(FP8X4),
+                        rhs_scale=v_scales[:, h * HD : (h + 1) * HD],
+                        start=True,
+                        stop=True,
+                    )
+            inv_sum = work.tile([P, 2, H], F32)
+            nc.vector.reciprocal(out=inv_sum[:], in_=row_sum[:])
+            o_sb = work.tile([P, 2, H, HD], F32)
+            nc.vector.tensor_tensor(
+                out=o_sb[:], in0=o_ps[:], in1=inv_sum[:].unsqueeze(3).to_broadcast([P, 2, H, HD]), op=ALU.mult
+            )
+            rows = out[b, 2 * pair * P : (2 * pair + 2) * P, :]
+            nc.sync.dma_start(out=rows.rearrange("(t p) n -> p t n", p=P), in_=o_sb[:].rearrange("p t h d -> p t (h d)"))
+
+        ready = prepare(0)
+        for b in range(B):
+            following = prepare(b + 1) if b + 1 < B else None
+            for pair in range(PAIRS):
+                attend(b, pair, ready)
+            ready = following

@@ -17,10 +17,10 @@ E = H * HD
 P = 128
 NT = S // P
 PACK = 4
-PAIRS = NT // 2
 EPS = 1e-5
 ROOT_HD = HD**0.5
-SPAN = 2 * S - P
+AHEAD = 1
+STEPS = 4
 
 FLOPS = 2 * B * S * D * E + 2 * (2 * B * H * S * S * HD)
 
@@ -30,12 +30,13 @@ def tile_bayesianattention_pa_t_kernel(tc, x, wv_words, wv_scales, q, k, mask, s
     with ExitStack() as ctx:
         const = ctx.enter_context(tc.tile_pool(name="const", bufs=1))
         inputs = ctx.enter_context(tc.tile_pool(name="inputs", bufs=B))
-        batch = ctx.enter_context(tc.tile_pool(name="batch", bufs=2))
+        batch = ctx.enter_context(tc.tile_pool(name="batch", bufs=AHEAD + 1))
         work = ctx.enter_context(tc.tile_pool(name="work", bufs=3))
+        stats = ctx.enter_context(tc.tile_pool(name="stats", bufs=6))
+        results = ctx.enter_context(tc.tile_pool(name="results", bufs=4))
         prep_psum = ctx.enter_context(tc.psum_pool(name="prep_psum", bufs=2))
         score_psum = ctx.enter_context(tc.psum_pool(name="score_psum", bufs=2))
-        turned_psum = ctx.enter_context(tc.psum_pool(name="turned_psum", bufs=2))
-        out_psum = ctx.enter_context(tc.psum_pool(name="out_psum", bufs=2))
+        fixed_psum = ctx.enter_context(tc.psum_pool(name="fixed_psum", bufs=1))
 
         shape_bf = const.tile([P, H], BF16)
         scale_bf = const.tile([P, H], BF16)
@@ -77,8 +78,11 @@ def tile_bayesianattention_pa_t_kernel(tc, x, wv_words, wv_scales, q, k, mask, s
         ident_bf = const.tile([P, P], BF16)
         make_identity(nc, ident_bf[:])
 
-        dist = const.tile([P, SPAN], I32)
-        nc.gpsimd.iota(dist[:], pattern=[[-1, SPAN]], base=S - P, channel_multiplier=1)
+        e_sb = const.tile([P, NT, H, S], BF16)
+        nc.vector.memset(e_sb[:].rearrange("p t h j -> p (t h j)").bitcast(I32), 0)
+
+        dist = const.tile([P, S], I32)
+        nc.gpsimd.iota(dist[:], pattern=[[-1, S]], base=0, channel_multiplier=1)
         eps_col = const.tile([P, 1], F32)
         nc.vector.memset(eps_col[:], EPS)
         shape_f = const.tile([P, H], F32)
@@ -92,7 +96,7 @@ def tile_bayesianattention_pa_t_kernel(tc, x, wv_words, wv_scales, q, k, mask, s
         offset = const.tile([P, H], F32)
         nc.vector.tensor_sub(out=offset[:], in0=exp_loc[:], in1=exp_neg_loc[:])
 
-        z = const.tile([P, H, SPAN], F32)
+        z = const.tile([P, H, S], F32)
         for h in range(H):
             nc.vector.tensor_scalar(
                 out=z[:, h, :], in0=dist[:], scalar1=offset[:, h : h + 1], scalar2=slope[:, h : h + 1],
@@ -100,7 +104,7 @@ def tile_bayesianattention_pa_t_kernel(tc, x, wv_words, wv_scales, q, k, mask, s
             )
         nc.scalar.activation(out=z[:], in_=z[:], func=ACT.Abs)
         nc.scalar.activation(out=z[:], in_=z[:], func=ACT.Ln, bias=eps_col[:])
-        power = const.tile([P, H, SPAN], F32)
+        power = const.tile([P, H, S], F32)
         for h in range(H):
             nc.scalar.activation(out=power[:, h, :], in_=z[:, h, :], func=ACT.Exp, scale=shape_f[:, h : h + 1])
 
@@ -110,141 +114,195 @@ def tile_bayesianattention_pa_t_kernel(tc, x, wv_words, wv_scales, q, k, mask, s
             mask_t = prep_psum.tile([P, 2, S], BF16, tag="prep")
             for jj in range(2):
                 jt = 2 * half + jj
-                for it in range(NT):
+                for it in range(jt, NT):
                     nc.tensor.transpose(
                         mask_t[:, jj, it * P : (it + 1) * P], mask_sb[:, it, jt * P : (jt + 1) * P], ident_bf[:]
                     )
-            nc.scalar.activation(
-                out=mask_scaled[:, 2 * half : 2 * half + 2, :], in_=mask_t[:], func=ACT.Copy, scale=ROOT_HD
-            )
+                nc.scalar.activation(
+                    out=mask_scaled[:, jt, jt * P :], in_=mask_t[:, jj, jt * P :], func=ACT.Copy, scale=ROOT_HD
+                )
         for h in range(H):
             for jt in range(NT):
-                first = S - P - P * jt
                 nc.vector.scalar_tensor_tensor(
-                    out=table[:, h, jt, :], in0=power[:, h, first : first + S], scalar=-ROOT_HD,
-                    in1=mask_scaled[:, jt, :], op0=ALU.mult, op1=ALU.add,
+                    out=table[:, h, jt, jt * P :], in0=power[:, h, : S - jt * P], scalar=-ROOT_HD,
+                    in1=mask_scaled[:, jt, jt * P :], op0=ALU.mult, op1=ALU.add,
                 )
 
-        def prepare(b):
-            turned = []
-            for name, rows in (("q_t", q_sb[b]), ("k_t", k_sb[b])):
+        x_grouped, x_codes, x_scales, v_grouped = {}, {}, {}, {}
+        q_t, k_t, v_codes, v_scales = {}, {}, {}, {}
+
+        def turn_x(b, half):
+            if half == 0:
+                x_grouped[b] = batch.tile([P, PACK, P, PACK], BF16, name="x_grouped", align_bytes=64)
+            x_words = x_sb[b][:].bitcast(F32)
+            grouped_words = (
+                x_grouped[b][:].rearrange("p t r c -> p (t r c)").bitcast(F32).rearrange("p (t r f) -> p t r f", t=PACK, f=2)
+            )
+            x_ps = prep_psum.tile([P, 2, 2, P], F32, tag="prep")
+            for tt in range(2):
+                for f in range(2):
+                    nc.tensor.transpose(x_ps[:, tt, f, :], x_words[:, 2 * half + tt, f : D // 2 : 2], ident_f32[:])
+            nc.vector.tensor_copy(
+                out=grouped_words[:, 2 * half : 2 * half + 2, :, :], in_=x_ps[:].rearrange("p t f r -> p t r f")
+            )
+
+        def quantise_x(b):
+            x_codes[b] = batch.tile([P, PACK * P], U32, name="x_codes", align_bytes=64)
+            x_scales[b] = batch.tile([P, PACK * P], U8, name="x_scales", align_bytes=64)
+            nc.vector.quantize_mx(
+                out=x_codes[b][:].bitcast(FP8X4), scales=x_scales[b][:],
+                in_=x_grouped[b][:].rearrange("p t r c -> p (t r c)"),
+            )
+
+        def turn_qk(b):
+            for name, rows, turned in (("q_t", q_sb[b], q_t), ("k_t", k_sb[b], k_t)):
                 t_ps = prep_psum.tile([P, H, S], BF16, tag="prep")
                 for h in range(H):
                     for t in range(NT):
                         nc.tensor.transpose(
                             t_ps[:, h, t * P : (t + 1) * P], rows[:, t, h * HD : (h + 1) * HD], ident_bf[:]
                         )
-                t_sb = batch.tile([P, H, S], BF16, name=name)
-                nc.scalar.copy(out=t_sb[:], in_=t_ps[:])
-                turned.append(t_sb)
+                turned[b] = batch.tile([P, H, S], BF16, name=name)
+                nc.scalar.copy(out=turned[b][:], in_=t_ps[:])
 
-            x_words = x_sb[b][:].bitcast(F32)
-            x_grouped = batch.tile([P, PACK, P, PACK], BF16, align_bytes=64)
-            x_grouped_words = (
-                x_grouped[:].rearrange("p t r c -> p (t r c)").bitcast(F32).rearrange("p (t r f) -> p t r f", t=PACK, f=2)
-            )
-            for half in range(2):
-                x_ps = prep_psum.tile([P, 2, 2, P], F32, tag="prep")
-                for tt in range(2):
-                    for f in range(2):
-                        nc.tensor.transpose(x_ps[:, tt, f, :], x_words[:, 2 * half + tt, f : D // 2 : 2], ident_f32[:])
-                nc.vector.tensor_copy(
-                    out=x_grouped_words[:, 2 * half : 2 * half + 2, :, :], in_=x_ps[:].rearrange("p t f r -> p t r f")
-                )
-            x_codes = batch.tile([P, PACK * P], U32, align_bytes=64)
-            x_scales = batch.tile([P, PACK * P], U8, align_bytes=64)
-            nc.vector.quantize_mx(
-                out=x_codes[:].bitcast(FP8X4), scales=x_scales[:], in_=x_grouped[:].rearrange("p t r c -> p (t r c)")
-            )
-
-            v_grouped = batch.tile([P, H, HD, PACK], BF16, align_bytes=64)
+        def project_v(b):
+            v_grouped[b] = batch.tile([P, H, HD, PACK], BF16, name="v_grouped", align_bytes=64)
             for h in range(H):
                 v_ps = prep_psum.tile([P, PACK, HD], F32, tag="prep")
                 for t in range(PACK):
                     nc.tensor.matmul_mx(
                         out=v_ps[:, t, :],
-                        lhsT=x_codes[:, t * P : (t + 1) * P].bitcast(FP8X4),
-                        lhsT_scale=x_scales[:, t * P : (t + 1) * P],
+                        lhsT=x_codes[b][:, t * P : (t + 1) * P].bitcast(FP8X4),
+                        lhsT_scale=x_scales[b][:, t * P : (t + 1) * P],
                         rhs=w_codes[:, h * HD : (h + 1) * HD].bitcast(FP8X4),
                         rhs_scale=w_scales[:, h * HD : (h + 1) * HD],
                         start=True,
                         stop=True,
                     )
-                nc.scalar.copy(out=v_grouped[:, h, :, :], in_=v_ps[:].rearrange("p t d -> p d t"))
-            v_codes = batch.tile([P, E], U32, align_bytes=64)
-            v_scales = batch.tile([P, E], U8, align_bytes=64)
+                nc.scalar.copy(out=v_grouped[b][:, h, :, :], in_=v_ps[:].rearrange("p t d -> p d t"))
+
+        def quantise_v(b):
+            v_codes[b] = batch.tile([P, E], U32, name="v_codes", align_bytes=64)
+            v_scales[b] = batch.tile([P, E], U8, name="v_scales", align_bytes=64)
             nc.vector.quantize_mx(
-                out=v_codes[:].bitcast(FP8X4), scales=v_scales[:], in_=v_grouped[:].rearrange("p h d t -> p (h d t)")
+                out=v_codes[b][:].bitcast(FP8X4), scales=v_scales[b][:],
+                in_=v_grouped[b][:].rearrange("p h d t -> p (h d t)"),
             )
-            return turned[0], turned[1], v_codes, v_scales
 
-        def attend(b, pair, ready):
-            q_t, k_t, v_codes, v_scales = ready
-            neg_max = work.tile([P, 2, H], F32)
-            row_sum = work.tile([P, 2, H], F32)
-            o_ps = out_psum.tile([P, 2, H, HD], F32)
-            for h in range(H):
-                e_ps = turned_psum.tile([P, 2, 2, P], F32)
-                for ii in range(2):
-                    it = 2 * pair + ii
-                    s_ps = score_psum.tile([P, S], F32)
+        def prepare(b, step):
+            if step == 0:
+                turn_x(b, 0)
+            elif step == 1:
+                turn_x(b, 1)
+            elif step == 2:
+                quantise_x(b)
+                turn_qk(b)
+            elif step == 3:
+                project_v(b)
+            else:
+                quantise_v(b)
+
+        groups = [(b, pair, h) for b in range(B) for h in range(H) for pair in (1, 0)]
+        e_ps = [fixed_psum.tile([P, 2, 2, P], F32, name="e_ps%d" % pair) for pair in range(2)]
+        o_ps = [fixed_psum.tile([P, 2, H, HD], F32, name="o_ps%d" % pair) for pair in range(2)]
+        neg_max, row_sum = {}, {}
+        e_grouped, e_codes, e_scales = {}, {}, {}
+
+        for ii in range(2):
+            nc.tensor.transpose(e_ps[0][:, ii, 1, :], e_sb[:, 0, 0, :].bitcast(F32)[:, P : 2 * P], ident_f32[:])
+
+        def scores_and_exp(n):
+            b, pair, h = groups[n]
+            if h == 0:
+                neg_max[b, pair] = stats.tile([P, 2, H], F32, name="neg_max")
+                row_sum[b, pair] = stats.tile([P, 2, H], F32, name="row_sum")
+            for ii in (1, 0):
+                it = 2 * pair + ii
+                keys = (it + 1) * P
+                s_ps = score_psum.tile([P, S], F32)
+                nc.tensor.matmul(
+                    out=s_ps[:, :keys], lhsT=q_t[b][:, h, it * P : (it + 1) * P], rhs=k_t[b][:, h, :keys],
+                    start=True, stop=False,
+                )
+                for jt in range(it + 1):
                     nc.tensor.matmul(
-                        out=s_ps[:], lhsT=q_t[:, h, it * P : (it + 1) * P], rhs=k_t[:, h, :], start=True, stop=False
+                        out=s_ps[:, jt * P : (jt + 1) * P],
+                        lhsT=table[:, h, jt, it * P : (it + 1) * P],
+                        rhs=ident_f32[:],
+                        is_transpose=True,
+                        start=False,
+                        stop=(jt == it),
                     )
-                    for jt in range(NT):
-                        nc.tensor.matmul(
-                            out=s_ps[:, jt * P : (jt + 1) * P],
-                            lhsT=table[:, h, jt, it * P : (it + 1) * P],
-                            rhs=ident_f32[:],
-                            is_transpose=True,
-                            start=False,
-                            stop=(jt == NT - 1),
-                        )
-                    neg_s = work.tile([P, S], F32)
-                    nc.vector.tensor_scalar(
-                        out=neg_s[:], in0=s_ps[:], scalar1=-1.0 / ROOT_HD, scalar2=None,
-                        op0=ALU.mult, op1=ALU.min, accum_out=neg_max[:, ii, h : h + 1],
-                    )
-                    e_sb = work.tile([P, S], BF16)
-                    nc.scalar.activation(
-                        out=e_sb[:], in_=neg_s[:], func=ACT.Exp, scale=-1.0, bias=neg_max[:, ii, h : h + 1],
-                        accum_out=row_sum[:, ii, h : h + 1],
-                    )
-                    e_words = e_sb[:].bitcast(F32)
-                    for u in range(2):
-                        nc.tensor.transpose(e_ps[:, ii, u, :], e_words[:, u * P : (u + 1) * P], ident_f32[:])
-                e_grouped = work.tile([P, 2, P, PACK], BF16, align_bytes=64)
-                nc.scalar.copy(
-                    out=e_grouped[:].rearrange("p t i c -> p (t i c)").bitcast(F32).rearrange("p (t i u) -> p t i u", t=2, u=2),
-                    in_=e_ps[:].rearrange("p t u i -> p t i u"),
+                neg_s = work.tile([P, S], F32)
+                nc.vector.tensor_scalar(
+                    out=neg_s[:, :keys], in0=s_ps[:, :keys], scalar1=-1.0 / ROOT_HD, scalar2=None,
+                    op0=ALU.mult, op1=ALU.min, accum_out=neg_max[b, pair][:, ii, h : h + 1],
                 )
-                e_codes = work.tile([P, 2 * P], U32, align_bytes=64)
-                e_scales = work.tile([P, 2 * P], U8, align_bytes=64)
-                nc.vector.quantize_mx(
-                    out=e_codes[:].bitcast(FP8X4), scales=e_scales[:], in_=e_grouped[:].rearrange("p t i c -> p (t i c)")
+                nc.scalar.activation(
+                    out=e_sb[:, it, h, :keys], in_=neg_s[:, :keys], func=ACT.Exp, scale=-1.0,
+                    bias=neg_max[b, pair][:, ii, h : h + 1], accum_out=row_sum[b, pair][:, ii, h : h + 1],
                 )
-                for ii in range(2):
-                    nc.tensor.matmul_mx(
-                        out=o_ps[:, ii, h, :],
-                        lhsT=e_codes[:, ii * P : (ii + 1) * P].bitcast(FP8X4),
-                        lhsT_scale=e_scales[:, ii * P : (ii + 1) * P],
-                        rhs=v_codes[:, h * HD : (h + 1) * HD].bitcast(FP8X4),
-                        rhs_scale=v_scales[:, h * HD : (h + 1) * HD],
-                        start=True,
-                        stop=True,
-                    )
-            inv_sum = work.tile([P, 2, H], F32)
-            nc.vector.reciprocal(out=inv_sum[:], in_=row_sum[:])
-            o_sb = work.tile([P, 2, H, HD], F32)
-            nc.vector.tensor_tensor(
-                out=o_sb[:], in0=o_ps[:], in1=inv_sum[:].unsqueeze(3).to_broadcast([P, 2, H, HD]), op=ALU.mult
-            )
-            rows = out[b, 2 * pair * P : (2 * pair + 2) * P, :]
-            nc.sync.dma_start(out=rows.rearrange("(t p) n -> p t n", p=P), in_=o_sb[:].rearrange("p t h d -> p t (h d)"))
 
-        ready = prepare(0)
-        for b in range(B):
-            following = prepare(b + 1) if b + 1 < B else None
-            for pair in range(PAIRS):
-                attend(b, pair, ready)
-            ready = following
+        def turn_e(n):
+            b, pair, h = groups[n]
+            for ii in range(2):
+                e_words = e_sb[:, 2 * pair + ii, h, :].bitcast(F32)
+                for u in range(pair + 1):
+                    nc.tensor.transpose(e_ps[pair][:, ii, u, :], e_words[:, u * P : (u + 1) * P], ident_f32[:])
+            e_grouped[n] = work.tile([P, 2, P, PACK], BF16, name="e_grouped", align_bytes=64)
+            nc.scalar.copy(
+                out=e_grouped[n][:].rearrange("p t i c -> p (t i c)").bitcast(F32).rearrange("p (t i u) -> p t i u", t=2, u=2),
+                in_=e_ps[pair][:].rearrange("p t u i -> p t i u"),
+            )
+
+        def quantise_e(n):
+            e_codes[n] = work.tile([P, 2 * P], U32, name="e_codes", align_bytes=64)
+            e_scales[n] = work.tile([P, 2 * P], U8, name="e_scales", align_bytes=64)
+            nc.vector.quantize_mx(
+                out=e_codes[n][:].bitcast(FP8X4), scales=e_scales[n][:],
+                in_=e_grouped[n][:].rearrange("p t i c -> p (t i c)"),
+            )
+
+        def multiply_and_store(n):
+            b, pair, h = groups[n]
+            for ii in range(2):
+                nc.tensor.matmul_mx(
+                    out=o_ps[pair][:, ii, h, :],
+                    lhsT=e_codes[n][:, ii * P : (ii + 1) * P].bitcast(FP8X4),
+                    lhsT_scale=e_scales[n][:, ii * P : (ii + 1) * P],
+                    rhs=v_codes[b][:, h * HD : (h + 1) * HD].bitcast(FP8X4),
+                    rhs_scale=v_scales[b][:, h * HD : (h + 1) * HD],
+                    start=True,
+                    stop=True,
+                )
+            if h == H - 1:
+                inv_sum = stats.tile([P, 2, H], F32)
+                nc.vector.reciprocal(out=inv_sum[:], in_=row_sum[b, pair][:])
+                o_sb = results.tile([P, 2, H, HD], F32)
+                nc.vector.tensor_tensor(
+                    out=o_sb[:], in0=o_ps[pair][:], in1=inv_sum[:].unsqueeze(3).to_broadcast([P, 2, H, HD]), op=ALU.mult
+                )
+                rows = out[b, 2 * pair * P : (2 * pair + 2) * P, :]
+                nc.sync.dma_start(
+                    out=rows.rearrange("(t p) n -> p t n", p=P), in_=o_sb[:].rearrange("p t h d -> p t (h d)")
+                )
+
+        for b in range(AHEAD):
+            for step in range(STEPS + 1):
+                prepare(b, step)
+
+        with tc.manual_schedule():
+            for n in range(len(groups) + 3):
+                if n < len(groups):
+                    scores_and_exp(n)
+                if 0 <= n - 1 < len(groups):
+                    turn_e(n - 1)
+                if 0 <= n - 2 < len(groups):
+                    quantise_e(n - 2)
+                if 0 <= n - 3 < len(groups):
+                    multiply_and_store(n - 3)
+                later, step = n // STEPS + AHEAD, n % STEPS
+                if step == 0 and AHEAD < later <= B:
+                    prepare(later - 1, STEPS)
+                if later < B:
+                    prepare(later, step)

@@ -19,8 +19,8 @@ NT = S // P
 PACK = 4
 EPS = 1e-5
 ROOT_HD = HD**0.5
-AHEAD = 1
-STEPS = 4
+GROUPS = 4
+LEAD = 2 * GROUPS
 
 FLOPS = 2 * B * S * D * E + 2 * (2 * B * H * S * S * HD)
 
@@ -30,7 +30,7 @@ def tile_bayesianattention_pa_t_kernel(tc, x, wv_words, wv_scales, q, k, mask, s
     with ExitStack() as ctx:
         const = ctx.enter_context(tc.tile_pool(name="const", bufs=1))
         inputs = ctx.enter_context(tc.tile_pool(name="inputs", bufs=B))
-        batch = ctx.enter_context(tc.tile_pool(name="batch", bufs=AHEAD + 1))
+        batch = ctx.enter_context(tc.tile_pool(name="batch", bufs=3))
         work = ctx.enter_context(tc.tile_pool(name="work", bufs=3))
         stats = ctx.enter_context(tc.tile_pool(name="stats", bufs=6))
         results = ctx.enter_context(tc.tile_pool(name="results", bufs=4))
@@ -68,23 +68,27 @@ def tile_bayesianattention_pa_t_kernel(tc, x, wv_words, wv_scales, q, k, mask, s
                 out=w_scales[32 * quad : 32 * quad + 4, :].bitcast(I32),
                 in_=wv_scales[0, 4 * quad : 4 * quad + 4, :].bitcast(I32),
             )
-        mask_sb = const.tile([P, NT, S], BF16)
-        nc.sync.dma_start(out=mask_sb[:], in_=mask[0, 0].rearrange("(t p) j -> p t j", p=P))
+        mask_sb = const.tile([P, NT, P], BF16)
+        for t in range(NT):
+            nc.sync.dma_start(out=mask_sb[:, t, :], in_=mask[0, 0, t * P : (t + 1) * P, t * P : (t + 1) * P])
         for b in range(1, B):
             load_batch(b)
 
-        ident_f32 = const.tile([P, P], F32)
-        make_identity(nc, ident_f32[:])
+        dist = const.tile([P, S], F32)
+        nc.gpsimd.iota(dist[:], pattern=[[-1, S]], base=0, channel_multiplier=1, allow_small_or_imprecise_dtypes=True)
         ident_bf = const.tile([P, P], BF16)
         make_identity(nc, ident_bf[:])
+        ident_f32 = const.tile([P, P], F32)
+        make_identity(nc, ident_f32[:])
+
+        eps_col = const.tile([P, 1], F32)
+        nc.vector.memset(eps_col[:], EPS)
+        warm = const.tile([P, 1], F32)
+        nc.scalar.activation(out=warm[:], in_=eps_col[:], func=ACT.Exp)
 
         e_sb = const.tile([P, NT, H, S], BF16)
         nc.vector.memset(e_sb[:].rearrange("p t h j -> p (t h j)").bitcast(I32), 0)
 
-        dist = const.tile([P, S], I32)
-        nc.gpsimd.iota(dist[:], pattern=[[-1, S]], base=0, channel_multiplier=1)
-        eps_col = const.tile([P, 1], F32)
-        nc.vector.memset(eps_col[:], EPS)
         shape_f = const.tile([P, H], F32)
         nc.vector.tensor_copy(out=shape_f[:], in_=shape_bf[:])
         slope = const.tile([P, H], F32)
@@ -95,38 +99,36 @@ def tile_bayesianattention_pa_t_kernel(tc, x, wv_words, wv_scales, q, k, mask, s
         nc.scalar.activation(out=exp_neg_loc[:], in_=loc_bf[:], func=ACT.Exp, scale=-1.0)
         offset = const.tile([P, H], F32)
         nc.vector.tensor_sub(out=offset[:], in0=exp_loc[:], in1=exp_neg_loc[:])
+        shift = const.tile([P, H], F32)
+        nc.vector.scalar_tensor_tensor(
+            out=shift[:], in0=offset[:], scalar=-1.0, in1=slope[:], op0=ALU.mult, op1=ALU.mult
+        )
 
         z = const.tile([P, H, S], F32)
         for h in range(H):
-            nc.vector.tensor_scalar(
-                out=z[:, h, :], in0=dist[:], scalar1=offset[:, h : h + 1], scalar2=slope[:, h : h + 1],
-                op0=ALU.subtract, op1=ALU.mult,
+            nc.scalar.activation(
+                out=z[:, h, :], in_=dist[:], func=ACT.Abs, scale=slope[:, h : h + 1], bias=shift[:, h : h + 1]
             )
-        nc.scalar.activation(out=z[:], in_=z[:], func=ACT.Abs)
         nc.scalar.activation(out=z[:], in_=z[:], func=ACT.Ln, bias=eps_col[:])
         power = const.tile([P, H, S], F32)
         for h in range(H):
             nc.scalar.activation(out=power[:, h, :], in_=z[:, h, :], func=ACT.Exp, scale=shape_f[:, h : h + 1])
 
-        table = const.tile([P, H, NT, S], F32)
-        mask_scaled = const.tile([P, NT, S], F32)
-        for half in range(2):
-            mask_t = prep_psum.tile([P, 2, S], BF16, tag="prep")
-            for jj in range(2):
-                jt = 2 * half + jj
-                for it in range(jt, NT):
-                    nc.tensor.transpose(
-                        mask_t[:, jj, it * P : (it + 1) * P], mask_sb[:, it, jt * P : (jt + 1) * P], ident_bf[:]
-                    )
-                nc.scalar.activation(
-                    out=mask_scaled[:, jt, jt * P :], in_=mask_t[:, jj, jt * P :], func=ACT.Copy, scale=ROOT_HD
-                )
+        mask_t = prep_psum.tile([P, NT, P], BF16, tag="prep")
+        for t in range(NT):
+            nc.tensor.transpose(mask_t[:, t, :], mask_sb[:, t, :], ident_bf[:])
+        mask_scaled = const.tile([P, NT, P], F32)
+        nc.vector.tensor_scalar(out=mask_scaled[:], in0=mask_t[:], scalar1=ROOT_HD, scalar2=None, op0=ALU.mult)
+        prior_t = const.tile([P, H, S], F32)
+        diag_t = const.tile([P, H, NT, P], F32)
         for h in range(H):
-            for jt in range(NT):
-                nc.vector.scalar_tensor_tensor(
-                    out=table[:, h, jt, jt * P :], in0=power[:, h, : S - jt * P], scalar=-ROOT_HD,
-                    in1=mask_scaled[:, jt, jt * P :], op0=ALU.mult, op1=ALU.add,
-                )
+            nc.vector.scalar_tensor_tensor(
+                out=diag_t[:, h, :, :], in0=power[:, h, :P].unsqueeze(1).to_broadcast([P, NT, P]), scalar=-ROOT_HD,
+                in1=mask_scaled[:], op0=ALU.mult, op1=ALU.add,
+            )
+            nc.vector.tensor_scalar(
+                out=prior_t[:, h, :], in0=power[:, h, :], scalar1=-ROOT_HD, scalar2=None, op0=ALU.mult
+            )
 
         x_grouped, x_codes, x_scales, v_grouped = {}, {}, {}, {}
         q_t, k_t, v_codes, v_scales = {}, {}, {}, {}
@@ -154,32 +156,29 @@ def tile_bayesianattention_pa_t_kernel(tc, x, wv_words, wv_scales, q, k, mask, s
                 in_=x_grouped[b][:].rearrange("p t r c -> p (t r c)"),
             )
 
-        def turn_qk(b):
-            for name, rows, turned in (("q_t", q_sb[b], q_t), ("k_t", k_sb[b], k_t)):
-                t_ps = prep_psum.tile([P, H, S], BF16, tag="prep")
-                for h in range(H):
-                    for t in range(NT):
-                        nc.tensor.transpose(
-                            t_ps[:, h, t * P : (t + 1) * P], rows[:, t, h * HD : (h + 1) * HD], ident_bf[:]
-                        )
-                turned[b] = batch.tile([P, H, S], BF16, name=name)
-                nc.scalar.copy(out=turned[b][:], in_=t_ps[:])
-
-        def project_v(b):
-            v_grouped[b] = batch.tile([P, H, HD, PACK], BF16, name="v_grouped", align_bytes=64)
+        def turn_rows(b, name, rows, turned):
+            t_ps = prep_psum.tile([P, H, S], BF16, tag="prep")
             for h in range(H):
-                v_ps = prep_psum.tile([P, PACK, HD], F32, tag="prep")
-                for t in range(PACK):
-                    nc.tensor.matmul_mx(
-                        out=v_ps[:, t, :],
-                        lhsT=x_codes[b][:, t * P : (t + 1) * P].bitcast(FP8X4),
-                        lhsT_scale=x_scales[b][:, t * P : (t + 1) * P],
-                        rhs=w_codes[:, h * HD : (h + 1) * HD].bitcast(FP8X4),
-                        rhs_scale=w_scales[:, h * HD : (h + 1) * HD],
-                        start=True,
-                        stop=True,
-                    )
-                nc.scalar.copy(out=v_grouped[b][:, h, :, :], in_=v_ps[:].rearrange("p t d -> p d t"))
+                for t in range(NT):
+                    nc.tensor.transpose(t_ps[:, h, t * P : (t + 1) * P], rows[:, t, h * HD : (h + 1) * HD], ident_bf[:])
+            turned[b] = batch.tile([P, H, S], BF16, name=name)
+            nc.scalar.copy(out=turned[b][:], in_=t_ps[:])
+
+        def project_v(b, h):
+            if h == 0:
+                v_grouped[b] = batch.tile([P, H, HD, PACK], BF16, name="v_grouped", align_bytes=64)
+            v_ps = prep_psum.tile([P, PACK, HD], F32, tag="prep")
+            for t in range(PACK):
+                nc.tensor.matmul_mx(
+                    out=v_ps[:, t, :],
+                    lhsT=x_codes[b][:, t * P : (t + 1) * P].bitcast(FP8X4),
+                    lhsT_scale=x_scales[b][:, t * P : (t + 1) * P],
+                    rhs=w_codes[:, h * HD : (h + 1) * HD].bitcast(FP8X4),
+                    rhs_scale=w_scales[:, h * HD : (h + 1) * HD],
+                    start=True,
+                    stop=True,
+                )
+            nc.scalar.copy(out=v_grouped[b][:, h, :, :], in_=v_ps[:].rearrange("p t d -> p d t"))
 
         def quantise_v(b):
             v_codes[b] = batch.tile([P, E], U32, name="v_codes", align_bytes=64)
@@ -191,16 +190,24 @@ def tile_bayesianattention_pa_t_kernel(tc, x, wv_words, wv_scales, q, k, mask, s
 
         def prepare(b, step):
             if step == 0:
-                turn_x(b, 0)
+                turn_rows(b, "q_t", q_sb[b], q_t)
             elif step == 1:
-                turn_x(b, 1)
-            elif step == 2:
+                turn_rows(b, "k_t", k_sb[b], k_t)
+            elif step in (2, 3):
+                turn_x(b, step - 2)
+            elif step == 4:
                 quantise_x(b)
-                turn_qk(b)
-            elif step == 3:
-                project_v(b)
+            elif step in (5, 6):
+                project_v(b, step - 5)
             else:
                 quantise_v(b)
+
+        def prepare_in_round(n):
+            newer, phase = divmod(n + LEAD, GROUPS)
+            if 0 <= newer - 1 < B:
+                prepare(newer - 1, GROUPS + phase)
+            if newer < B:
+                prepare(newer, phase)
 
         groups = [(b, pair, h) for b in range(B) for h in range(H) for pair in (1, 0)]
         e_ps = [fixed_psum.tile([P, 2, 2, P], F32, name="e_ps%d" % pair) for pair in range(2)]
@@ -227,7 +234,7 @@ def tile_bayesianattention_pa_t_kernel(tc, x, wv_words, wv_scales, q, k, mask, s
                 for jt in range(it + 1):
                     nc.tensor.matmul(
                         out=s_ps[:, jt * P : (jt + 1) * P],
-                        lhsT=table[:, h, jt, it * P : (it + 1) * P],
+                        lhsT=diag_t[:, h, it, :] if jt == it else prior_t[:, h, (it - jt) * P : (it - jt + 1) * P],
                         rhs=ident_f32[:],
                         is_transpose=True,
                         start=False,
@@ -250,10 +257,13 @@ def tile_bayesianattention_pa_t_kernel(tc, x, wv_words, wv_scales, q, k, mask, s
                 for u in range(pair + 1):
                     nc.tensor.transpose(e_ps[pair][:, ii, u, :], e_words[:, u * P : (u + 1) * P], ident_f32[:])
             e_grouped[n] = work.tile([P, 2, P, PACK], BF16, name="e_grouped", align_bytes=64)
-            nc.scalar.copy(
-                out=e_grouped[n][:].rearrange("p t i c -> p (t i c)").bitcast(F32).rearrange("p (t i u) -> p t i u", t=2, u=2),
-                in_=e_ps[pair][:].rearrange("p t u i -> p t i u"),
+            grouped_words = (
+                e_grouped[n][:].rearrange("p t i c -> p (t i c)").bitcast(F32).rearrange("p (t i u) -> p t i u", t=2, u=2)
             )
+            if n % GROUPS == GROUPS - 1:
+                nc.vector.tensor_copy(out=grouped_words, in_=e_ps[pair][:].rearrange("p t u i -> p t i u"))
+            else:
+                nc.scalar.copy(out=grouped_words, in_=e_ps[pair][:].rearrange("p t u i -> p t i u"))
 
         def quantise_e(n):
             e_codes[n] = work.tile([P, 2 * P], U32, name="e_codes", align_bytes=64)
@@ -287,9 +297,8 @@ def tile_bayesianattention_pa_t_kernel(tc, x, wv_words, wv_scales, q, k, mask, s
                     out=rows.rearrange("(t p) n -> p t n", p=P), in_=o_sb[:].rearrange("p t h d -> p t (h d)")
                 )
 
-        for b in range(AHEAD):
-            for step in range(STEPS + 1):
-                prepare(b, step)
+        for n in range(-LEAD, 0):
+            prepare_in_round(n)
 
         with tc.manual_schedule():
             for n in range(len(groups) + 3):
@@ -301,8 +310,4 @@ def tile_bayesianattention_pa_t_kernel(tc, x, wv_words, wv_scales, q, k, mask, s
                     quantise_e(n - 2)
                 if 0 <= n - 3 < len(groups):
                     multiply_and_store(n - 3)
-                later, step = n // STEPS + AHEAD, n % STEPS
-                if step == 0 and AHEAD < later <= B:
-                    prepare(later - 1, STEPS)
-                if later < B:
-                    prepare(later, step)
+                prepare_in_round(n)

@@ -20,7 +20,7 @@ PACK = 4
 EPS = 1e-5
 ROOT_HD = HD**0.5
 GROUPS = 4
-LEAD = 2 * GROUPS
+LEAD = 7
 
 FLOPS = 2 * B * S * D * E + 2 * (2 * B * H * S * S * HD)
 
@@ -68,9 +68,6 @@ def tile_bayesianattention_pa_t_kernel(tc, x, wv_words, wv_scales, q, k, mask, s
                 out=w_scales[32 * quad : 32 * quad + 4, :].bitcast(I32),
                 in_=wv_scales[0, 4 * quad : 4 * quad + 4, :].bitcast(I32),
             )
-        mask_sb = const.tile([P, NT, P], BF16)
-        for t in range(NT):
-            nc.sync.dma_start(out=mask_sb[:, t, :], in_=mask[0, 0, t * P : (t + 1) * P, t * P : (t + 1) * P])
         for b in range(1, B):
             load_batch(b)
 
@@ -78,6 +75,8 @@ def tile_bayesianattention_pa_t_kernel(tc, x, wv_words, wv_scales, q, k, mask, s
         nc.gpsimd.iota(dist[:], pattern=[[-1, S]], base=0, channel_multiplier=1, allow_small_or_imprecise_dtypes=True)
         ident_bf = const.tile([P, P], BF16)
         make_identity(nc, ident_bf[:])
+        mask_sb = const.tile([P, NT, S], BF16)
+        nc.gpsimd.dma_start(out=mask_sb[:], in_=mask[0, 0].rearrange("(t p) j -> p t j", p=P))
         ident_f32 = const.tile([P, P], F32)
         make_identity(nc, ident_f32[:])
 
@@ -116,7 +115,7 @@ def tile_bayesianattention_pa_t_kernel(tc, x, wv_words, wv_scales, q, k, mask, s
 
         mask_t = prep_psum.tile([P, NT, P], BF16, tag="prep")
         for t in range(NT):
-            nc.tensor.transpose(mask_t[:, t, :], mask_sb[:, t, :], ident_bf[:])
+            nc.tensor.transpose(mask_t[:, t, :], mask_sb[:, t, t * P : (t + 1) * P], ident_bf[:])
         mask_scaled = const.tile([P, NT, P], F32)
         nc.vector.tensor_scalar(out=mask_scaled[:], in0=mask_t[:], scalar1=ROOT_HD, scalar2=None, op0=ALU.mult)
         prior_t = const.tile([P, H, S], F32)
@@ -197,22 +196,21 @@ def tile_bayesianattention_pa_t_kernel(tc, x, wv_words, wv_scales, q, k, mask, s
                 turn_x(b, step - 2)
             elif step == 4:
                 quantise_x(b)
-            elif step in (5, 6):
-                project_v(b, step - 5)
-            else:
+            elif step in (6, 8):
+                project_v(b, (step - 6) // 2)
+            elif step == 9:
                 quantise_v(b)
 
         def prepare_in_round(n):
-            newer, phase = divmod(n + LEAD, GROUPS)
-            if 0 <= newer - 1 < B:
-                prepare(newer - 1, GROUPS + phase)
-            if newer < B:
-                prepare(newer, phase)
+            newest, phase = divmod(n + LEAD, GROUPS)
+            for age in (2, 1, 0):
+                if 0 <= newest - age < B:
+                    prepare(newest - age, age * GROUPS + phase)
 
         groups = [(b, pair, h) for b in range(B) for h in range(H) for pair in (1, 0)]
         e_ps = [fixed_psum.tile([P, 2, 2, P], F32, name="e_ps%d" % pair) for pair in range(2)]
         o_ps = [fixed_psum.tile([P, 2, H, HD], F32, name="o_ps%d" % pair) for pair in range(2)]
-        neg_max, row_sum = {}, {}
+        neg_max, row_sum, inv_sum = {}, {}, {}
         e_grouped, e_codes, e_scales = {}, {}, {}
 
         for ii in range(2):
@@ -228,8 +226,7 @@ def tile_bayesianattention_pa_t_kernel(tc, x, wv_words, wv_scales, q, k, mask, s
                 keys = (it + 1) * P
                 s_ps = score_psum.tile([P, S], F32)
                 nc.tensor.matmul(
-                    out=s_ps[:, :keys], lhsT=q_t[b][:, h, it * P : (it + 1) * P], rhs=k_t[b][:, h, :keys],
-                    start=True, stop=False,
+                    out=s_ps[:], lhsT=q_t[b][:, h, it * P : (it + 1) * P], rhs=k_t[b][:, h, :], start=True, stop=False
                 )
                 for jt in range(it + 1):
                     nc.tensor.matmul(
@@ -260,18 +257,19 @@ def tile_bayesianattention_pa_t_kernel(tc, x, wv_words, wv_scales, q, k, mask, s
             grouped_words = (
                 e_grouped[n][:].rearrange("p t i c -> p (t i c)").bitcast(F32).rearrange("p (t i u) -> p t i u", t=2, u=2)
             )
-            if n % GROUPS == GROUPS - 1:
-                nc.vector.tensor_copy(out=grouped_words, in_=e_ps[pair][:].rearrange("p t u i -> p t i u"))
-            else:
-                nc.scalar.copy(out=grouped_words, in_=e_ps[pair][:].rearrange("p t u i -> p t i u"))
+            nc.scalar.copy(out=grouped_words, in_=e_ps[pair][:].rearrange("p t u i -> p t i u"))
 
         def quantise_e(n):
+            b, pair, h = groups[n]
             e_codes[n] = work.tile([P, 2 * P], U32, name="e_codes", align_bytes=64)
             e_scales[n] = work.tile([P, 2 * P], U8, name="e_scales", align_bytes=64)
             nc.vector.quantize_mx(
                 out=e_codes[n][:].bitcast(FP8X4), scales=e_scales[n][:],
                 in_=e_grouped[n][:].rearrange("p t i c -> p (t i c)"),
             )
+            if h == H - 1:
+                inv_sum[b, pair] = stats.tile([P, 2, H], F32, name="inv_sum")
+                nc.vector.reciprocal(out=inv_sum[b, pair][:], in_=row_sum[b, pair][:])
 
         def multiply_and_store(n):
             b, pair, h = groups[n]
@@ -286,11 +284,10 @@ def tile_bayesianattention_pa_t_kernel(tc, x, wv_words, wv_scales, q, k, mask, s
                     stop=True,
                 )
             if h == H - 1:
-                inv_sum = stats.tile([P, 2, H], F32)
-                nc.vector.reciprocal(out=inv_sum[:], in_=row_sum[b, pair][:])
                 o_sb = results.tile([P, 2, H, HD], F32)
                 nc.vector.tensor_tensor(
-                    out=o_sb[:], in0=o_ps[pair][:], in1=inv_sum[:].unsqueeze(3).to_broadcast([P, 2, H, HD]), op=ALU.mult
+                    out=o_sb[:], in0=o_ps[pair][:], in1=inv_sum[b, pair][:].unsqueeze(3).to_broadcast([P, 2, H, HD]),
+                    op=ALU.mult,
                 )
                 rows = out[b, 2 * pair * P : (2 * pair + 2) * P, :]
                 nc.sync.dma_start(
@@ -301,13 +298,15 @@ def tile_bayesianattention_pa_t_kernel(tc, x, wv_words, wv_scales, q, k, mask, s
             prepare_in_round(n)
 
         with tc.manual_schedule():
-            for n in range(len(groups) + 3):
+            for n in range(len(groups) + 5):
                 if n < len(groups):
                     scores_and_exp(n)
                 if 0 <= n - 1 < len(groups):
                     turn_e(n - 1)
                 if 0 <= n - 2 < len(groups):
                     quantise_e(n - 2)
-                if 0 <= n - 3 < len(groups):
-                    multiply_and_store(n - 3)
+                if n % 2 == 1:
+                    for m in (n - 4, n - 3):
+                        if 0 <= m < len(groups):
+                            multiply_and_store(m)
                 prepare_in_round(n)

@@ -301,8 +301,6 @@ def tile_bayesianattention_pa_t_kernel(tc, x, wv_words, wv_scales, q, k, mask, s
             for n in range(len(groups) + 5):
                 if n < len(groups):
                     scores_and_exp(n)
-                if 0 <= n - 1 < len(groups):
-                    turn_e(n - 1)
                 if 0 <= n - 2 < len(groups):
                     quantise_e(n - 2)
                 if n % 2 == 1:
@@ -310,3 +308,5 @@ def tile_bayesianattention_pa_t_kernel(tc, x, wv_words, wv_scales, q, k, mask, s
                         if 0 <= m < len(groups):
                             multiply_and_store(m)
                 prepare_in_round(n)
+                if 0 <= n - 1 < len(groups):
+                    turn_e(n - 1)

@@ -96,22 +96,25 @@ def tile_bayesianattention_pa_t_kernel(tc, x, wv_words, wv_scales, q, k, mask, s
         nc.scalar.activation(out=exp_loc[:], in_=loc_bf[:], func=ACT.Exp)
         exp_neg_loc = const.tile([P, H], F32)
         nc.scalar.activation(out=exp_neg_loc[:], in_=loc_bf[:], func=ACT.Exp, scale=-1.0)
+        nc.scalar.activation(out=warm[:], in_=exp_neg_loc[:, 0:1], func=ACT.Ln)
         offset = const.tile([P, H], F32)
         nc.vector.tensor_sub(out=offset[:], in0=exp_loc[:], in1=exp_neg_loc[:])
-        shift = const.tile([P, H], F32)
-        nc.vector.scalar_tensor_tensor(
-            out=shift[:], in0=offset[:], scalar=-1.0, in1=slope[:], op0=ALU.mult, op1=ALU.mult
-        )
 
         z = const.tile([P, H, S], F32)
+        abs_z = const.tile([P, H, S], F32)
+        log_z = const.tile([P, H, S], F32)
         for h in range(H):
-            nc.scalar.activation(
-                out=z[:, h, :], in_=dist[:], func=ACT.Abs, scale=slope[:, h : h + 1], bias=shift[:, h : h + 1]
+            nc.vector.tensor_scalar(
+                out=z[:, h, :], in0=dist[:], scalar1=offset[:, h : h + 1], scalar2=slope[:, h : h + 1],
+                op0=ALU.subtract, op1=ALU.mult,
             )
-        nc.scalar.activation(out=z[:], in_=z[:], func=ACT.Ln, bias=eps_col[:])
+            nc.vector.scalar_tensor_tensor(
+                out=abs_z[:, h, :], in0=z[:, h, :], scalar=-1.0, in1=z[:, h, :], op0=ALU.mult, op1=ALU.max
+            )
+            nc.scalar.activation(out=log_z[:, h, :], in_=abs_z[:, h, :], func=ACT.Ln, bias=eps_col[:])
         power = const.tile([P, H, S], F32)
         for h in range(H):
-            nc.scalar.activation(out=power[:, h, :], in_=z[:, h, :], func=ACT.Exp, scale=shape_f[:, h : h + 1])
+            nc.scalar.activation(out=power[:, h, :], in_=log_z[:, h, :], func=ACT.Exp, scale=shape_f[:, h : h + 1])
 
         mask_t = prep_psum.tile([P, NT, P], BF16, tag="prep")
         for t in range(NT):
@@ -155,13 +158,21 @@ def tile_bayesianattention_pa_t_kernel(tc, x, wv_words, wv_scales, q, k, mask, s
                 in_=x_grouped[b][:].rearrange("p t r c -> p (t r c)"),
             )
 
-        def turn_rows(b, name, rows, turned):
-            t_ps = prep_psum.tile([P, H, S], BF16, tag="prep")
-            for h in range(H):
-                for t in range(NT):
-                    nc.tensor.transpose(t_ps[:, h, t * P : (t + 1) * P], rows[:, t, h * HD : (h + 1) * HD], ident_bf[:])
-            turned[b] = batch.tile([P, H, S], BF16, name=name)
-            nc.scalar.copy(out=turned[b][:], in_=t_ps[:])
+        def turn_rows(b, piece):
+            name, rows, turned = ("q_t", q_sb[b], q_t) if piece < H else ("k_t", k_sb[b], k_t)
+            h = piece % H
+            if h == 0:
+                turned[b] = batch.tile([P, H, S], BF16, name=name)
+            t_ps = prep_psum.tile([P, S], BF16, tag="prep")
+            for t in range(NT):
+                nc.tensor.matmul(
+                    out=t_ps[:, t * P : (t + 1) * P], lhsT=rows[:, t, h * HD : (h + 1) * HD], rhs=ident_bf[:],
+                    start=True, stop=True,
+                )
+            if piece < 2 * H - 1:
+                nc.scalar.copy(out=turned[b][:, h, :], in_=t_ps[:])
+            else:
+                nc.vector.tensor_copy(out=turned[b][:, h, :], in_=t_ps[:])
 
         def project_v(b, h):
             if h == 0:
@@ -188,17 +199,15 @@ def tile_bayesianattention_pa_t_kernel(tc, x, wv_words, wv_scales, q, k, mask, s
             )
 
         def prepare(b, step):
-            if step == 0:
-                turn_rows(b, "q_t", q_sb[b], q_t)
-            elif step == 1:
-                turn_rows(b, "k_t", k_sb[b], k_t)
-            elif step in (2, 3):
-                turn_x(b, step - 2)
-            elif step == 4:
+            if step < 2 * H:
+                turn_rows(b, step)
+            if step in (1, 3):
+                turn_x(b, (step - 1) // 2)
+            if step == 4:
                 quantise_x(b)
-            elif step in (6, 8):
+            if step in (6, 8):
                 project_v(b, (step - 6) // 2)
-            elif step == 9:
+            if step == 9:
                 quantise_v(b)
 
         def prepare_in_round(n):
@@ -226,7 +235,8 @@ def tile_bayesianattention_pa_t_kernel(tc, x, wv_words, wv_scales, q, k, mask, s
                 keys = (it + 1) * P
                 s_ps = score_psum.tile([P, S], F32)
                 nc.tensor.matmul(
-                    out=s_ps[:], lhsT=q_t[b][:, h, it * P : (it + 1) * P], rhs=k_t[b][:, h, :], start=True, stop=False
+                    out=s_ps[:, :keys], lhsT=q_t[b][:, h, it * P : (it + 1) * P], rhs=k_t[b][:, h, :keys],
+                    start=True, stop=False,
                 )
                 for jt in range(it + 1):
                     nc.tensor.matmul(
@@ -301,10 +311,10 @@ def tile_bayesianattention_pa_t_kernel(tc, x, wv_words, wv_scales, q, k, mask, s
             for n in range(len(groups) + 5):
                 if n < len(groups):
                     scores_and_exp(n)
-                if 0 <= n - 2 < len(groups):
-                    quantise_e(n - 2)
+                if 0 <= n - 3 < len(groups):
+                    quantise_e(n - 3)
                 if n % 2 == 1:
-                    for m in (n - 4, n - 3):
+                    for m in (n - 5, n - 4):
                         if 0 <= m < len(groups):
                             multiply_and_store(m)
                 prepare_in_round(n)

@@ -234,19 +234,19 @@ def tile_bayesianattention_pa_t_kernel(tc, x, wv_words, wv_scales, q, k, mask, s
                 it = 2 * pair + ii
                 keys = (it + 1) * P
                 s_ps = score_psum.tile([P, S], F32)
-                nc.tensor.matmul(
-                    out=s_ps[:, :keys], lhsT=q_t[b][:, h, it * P : (it + 1) * P], rhs=k_t[b][:, h, :keys],
-                    start=True, stop=False,
-                )
                 for jt in range(it + 1):
                     nc.tensor.matmul(
                         out=s_ps[:, jt * P : (jt + 1) * P],
                         lhsT=diag_t[:, h, it, :] if jt == it else prior_t[:, h, (it - jt) * P : (it - jt + 1) * P],
                         rhs=ident_f32[:],
                         is_transpose=True,
-                        start=False,
-                        stop=(jt == it),
+                        start=(jt == 0),
+                        stop=False,
                     )
+                nc.tensor.matmul(
+                    out=s_ps[:, :keys], lhsT=q_t[b][:, h, it * P : (it + 1) * P], rhs=k_t[b][:, h, :keys],
+                    start=False, stop=True,
+                )
                 neg_s = work.tile([P, S], F32)
                 nc.vector.tensor_scalar(
                     out=neg_s[:, :keys], in0=s_ps[:, :keys], scalar1=-1.0 / ROOT_HD, scalar2=None,

@@ -1,3 +1,4 @@
+import math
 from contextlib import ExitStack
 
 import concourse.mybir as mybir
@@ -11,16 +12,22 @@ U8 = mybir.dt.uint8
 FP8X4 = mybir.dt.float8_e4m3fn_x4
 ALU = mybir.AluOpType
 ACT = mybir.ActivationFunctionType
+AX = mybir.AxisListType
 
 B, S, D, H, HD = 8, 512, 512, 2, 128
 E = H * HD
 P = 128
+HALF = P // 2
 NT = S // P
 PACK = 4
 EPS = 1e-5
 ROOT_HD = HD**0.5
-GROUPS = 4
-LEAD = 7
+TWIN = 2
+RING = 3
+GROUPS = 6
+LEAD = 6
+
+KEY_TILE = ((0, 2, 1, 3), (3, 0, 2, 1))
 
 FLOPS = 2 * B * S * D * E + 2 * (2 * B * H * S * S * HD)
 
@@ -30,125 +37,186 @@ def tile_bayesianattention_pa_t_kernel(tc, x, wv_words, wv_scales, q, k, mask, s
     with ExitStack() as ctx:
         const = ctx.enter_context(tc.tile_pool(name="const", bufs=1))
         inputs = ctx.enter_context(tc.tile_pool(name="inputs", bufs=B))
-        batch = ctx.enter_context(tc.tile_pool(name="batch", bufs=3))
-        work = ctx.enter_context(tc.tile_pool(name="work", bufs=3))
-        stats = ctx.enter_context(tc.tile_pool(name="stats", bufs=6))
-        results = ctx.enter_context(tc.tile_pool(name="results", bufs=4))
-        prep_psum = ctx.enter_context(tc.psum_pool(name="prep_psum", bufs=2))
-        score_psum = ctx.enter_context(tc.psum_pool(name="score_psum", bufs=2))
-        fixed_psum = ctx.enter_context(tc.psum_pool(name="fixed_psum", bufs=1))
+        batch = ctx.enter_context(tc.tile_pool(name="batch", bufs=4))
+        twins = ctx.enter_context(tc.tile_pool(name="twins", bufs=2))
+        work = ctx.enter_context(tc.tile_pool(name="work", bufs=5))
+        stats = ctx.enter_context(tc.tile_pool(name="stats", bufs=8))
+        results = ctx.enter_context(tc.tile_pool(name="results", bufs=3))
+        score_psum = ctx.enter_context(tc.psum_pool(name="score_psum", bufs=3))
+        ring_psum = ctx.enter_context(tc.psum_pool(name="ring_psum", bufs=3))
+        o_psum = ctx.enter_context(tc.psum_pool(name="o_psum", bufs=2))
+        ctx.enter_context(tc.manual_schedule())
 
+        w_scales = const.tile([P, E], U8, align_bytes=64)
+        nc.vector.memset(w_scales[:].bitcast(I32), 0)
         shape_bf = const.tile([P, H], BF16)
         scale_bf = const.tile([P, H], BF16)
         loc_bf = const.tile([P, H], BF16)
-        for dst, src in ((shape_bf, shape), (scale_bf, scale), (loc_bf, loc)):
+        for dst, src in ((scale_bf, scale), (loc_bf, loc), (shape_bf, shape)):
             nc.scalar.dma_start(out=dst[:], in_=src.rearrange("a h b c -> (a h b c)").partition_broadcast(P))
 
         q_sb, k_sb, x_sb = [], [], []
 
         def load_batch(b):
-            q_sb.append(inputs.tile([P, NT, E], BF16, name="q_sb"))
-            nc.sync.dma_start(out=q_sb[b][:], in_=q[b].rearrange("(t p) h d -> p t (h d)", p=P))
             k_sb.append(inputs.tile([P, NT, E], BF16, name="k_sb"))
             nc.sync.dma_start(out=k_sb[b][:], in_=k[b].rearrange("(t p) h d -> p t (h d)", p=P))
+            q_sb.append(inputs.tile([P, NT, E], BF16, name="q_sb"))
+            nc.sync.dma_start(out=q_sb[b][:], in_=q[b].rearrange("(t p) h d -> p t (h d)", p=P))
             x_sb.append(inputs.tile([P, PACK, D], BF16, name="x_sb"))
-            nc.sync.dma_start(
-                out=x_sb[b][:].rearrange("p (u e) c -> p u (e c)", u=2),
-                in_=x[b].rearrange("(u p e) c -> p u (e c)", u=2, e=2),
-            )
+            for half in range(2):
+                rows = x_sb[b][half * HALF : (half + 1) * HALF, :, :].rearrange("p (u e) c -> p u (e c)", u=2)
+                tiles = KEY_TILE[b % TWIN][half], KEY_TILE[b % TWIN][half + 2]
+                if tiles[1] == tiles[0] + 1:
+                    src = x[b, tiles[0] * P : (tiles[0] + 2) * P, :].rearrange("(u p e) c -> p u (e c)", u=2, e=2)
+                    nc.sync.dma_start(out=rows, in_=src)
+                else:
+                    for u in range(2):
+                        src = x[b, tiles[u] * P : (tiles[u] + 1) * P, :].rearrange("(p e) c -> p (e c)", e=2)
+                        nc.sync.dma_start(out=rows[:, u, :], in_=src)
 
         load_batch(0)
+        mask_sb = const.tile([P, NT, P], BF16)
+        for t in range(NT):
+            nc.sync.dma_start(out=mask_sb[:, t, :], in_=mask[0, 0, t * P : (t + 1) * P, t * P : (t + 1) * P])
 
+        load_batch(1)
         w_codes = const.tile([P, E], U32, align_bytes=64)
-        w_scales = const.tile([P, E], U8, align_bytes=64)
-        nc.vector.memset(w_scales[:].bitcast(I32), 0)
         nc.sync.dma_start(out=w_codes[:].bitcast(I32), in_=wv_words[0].rearrange("p n t -> p (n t)").bitcast(I32))
         for quad in range(4):
             nc.sync.dma_start(
                 out=w_scales[32 * quad : 32 * quad + 4, :].bitcast(I32),
                 in_=wv_scales[0, 4 * quad : 4 * quad + 4, :].bitcast(I32),
             )
-        for b in range(1, B):
+        for b in range(2, B):
             load_batch(b)
-
-        dist = const.tile([P, S], F32)
-        nc.gpsimd.iota(dist[:], pattern=[[-1, S]], base=0, channel_multiplier=1, allow_small_or_imprecise_dtypes=True)
-        ident_bf = const.tile([P, P], BF16)
-        make_identity(nc, ident_bf[:])
-        mask_sb = const.tile([P, NT, S], BF16)
-        nc.gpsimd.dma_start(out=mask_sb[:], in_=mask[0, 0].rearrange("(t p) j -> p t j", p=P))
-        ident_f32 = const.tile([P, P], F32)
-        make_identity(nc, ident_f32[:])
 
         eps_col = const.tile([P, 1], F32)
         nc.vector.memset(eps_col[:], EPS)
         warm = const.tile([P, 1], F32)
         nc.scalar.activation(out=warm[:], in_=eps_col[:], func=ACT.Exp)
+        log_root = const.tile([P, 1], F32)
+        nc.vector.tensor_scalar(
+            out=log_root[:], in0=eps_col[:], scalar1=0.0, scalar2=math.log(ROOT_HD), op0=ALU.mult, op1=ALU.add
+        )
+        ident_f32 = const.tile([P, P], F32)
+        make_identity(nc, ident_f32[:])
+        ident_bf = const.tile([P, P], BF16)
+        nc.vector.tensor_copy(out=ident_bf[:], in_=ident_f32[:])
+        minus_ident_bf = const.tile([P, P], BF16)
+        nc.vector.tensor_scalar(
+            out=minus_ident_bf[:], in0=ident_f32[:], scalar1=-1.0, scalar2=None, op0=ALU.mult
+        )
+        dist = const.tile([P, S], F32)
+        nc.gpsimd.iota(dist[:], pattern=[[-1, S]], base=0, channel_multiplier=1, allow_small_or_imprecise_dtypes=True)
 
-        e_sb = const.tile([P, NT, H, S], BF16)
-        nc.vector.memset(e_sb[:].rearrange("p t h j -> p (t h j)").bitcast(I32), 0)
+        e_long, e_short = {}, []
+        for h in range(H):
+            for j in range(TWIN):
+                e_long[j, h] = const.tile([P, 2, NT, P], BF16, name="e_long%d%d" % (j, h))
+                dead = KEY_TILE[j].index(NT - 1)
+                nc.vector.memset(e_long[j, h][:, 0, dead, :].bitcast(I32), 0)
+            e_short.append(const.tile([P, 2, NT, P], BF16, name="e_short%d" % h))
+            nc.vector.memset(e_short[h][:, 0, 2:NT, :].rearrange("p t c -> p (t c)").bitcast(I32), 0)
+        v_masked = [const.tile([P, H, TWIN, HD], U32, name="v_masked%d" % i, align_bytes=64) for i in range(2)]
+        for i in range(2):
+            nc.vector.memset(v_masked[i][:].rearrange("p h j d -> p (h j d)").bitcast(I32), 0)
 
-        shape_f = const.tile([P, H], F32)
-        nc.vector.tensor_copy(out=shape_f[:], in_=shape_bf[:])
         slope = const.tile([P, H], F32)
-        nc.scalar.activation(out=slope[:], in_=scale_bf[:], func=ACT.Exp)
         exp_loc = const.tile([P, H], F32)
-        nc.scalar.activation(out=exp_loc[:], in_=loc_bf[:], func=ACT.Exp)
         exp_neg_loc = const.tile([P, H], F32)
-        nc.scalar.activation(out=exp_neg_loc[:], in_=loc_bf[:], func=ACT.Exp, scale=-1.0)
-        nc.scalar.activation(out=warm[:], in_=exp_neg_loc[:, 0:1], func=ACT.Ln)
+        shape_f = const.tile([P, H], F32)
         offset = const.tile([P, H], F32)
-        nc.vector.tensor_sub(out=offset[:], in0=exp_loc[:], in1=exp_neg_loc[:])
-
         z = const.tile([P, H, S], F32)
         abs_z = const.tile([P, H, S], F32)
         log_z = const.tile([P, H, S], F32)
-        for h in range(H):
-            nc.vector.tensor_scalar(
-                out=z[:, h, :], in0=dist[:], scalar1=offset[:, h : h + 1], scalar2=slope[:, h : h + 1],
-                op0=ALU.subtract, op1=ALU.mult,
-            )
-            nc.vector.scalar_tensor_tensor(
-                out=abs_z[:, h, :], in0=z[:, h, :], scalar=-1.0, in1=z[:, h, :], op0=ALU.mult, op1=ALU.max
-            )
-            nc.scalar.activation(out=log_z[:, h, :], in_=abs_z[:, h, :], func=ACT.Ln, bias=eps_col[:])
-        power = const.tile([P, H, S], F32)
-        for h in range(H):
-            nc.scalar.activation(out=power[:, h, :], in_=log_z[:, h, :], func=ACT.Exp, scale=shape_f[:, h : h + 1])
-
-        mask_t = prep_psum.tile([P, NT, P], BF16, tag="prep")
-        for t in range(NT):
-            nc.tensor.transpose(mask_t[:, t, :], mask_sb[:, t, t * P : (t + 1) * P], ident_bf[:])
-        mask_scaled = const.tile([P, NT, P], F32)
-        nc.vector.tensor_scalar(out=mask_scaled[:], in0=mask_t[:], scalar1=ROOT_HD, scalar2=None, op0=ALU.mult)
         prior_t = const.tile([P, H, S], F32)
         diag_t = const.tile([P, H, NT, P], F32)
-        for h in range(H):
-            nc.vector.scalar_tensor_tensor(
-                out=diag_t[:, h, :, :], in0=power[:, h, :P].unsqueeze(1).to_broadcast([P, NT, P]), scalar=-ROOT_HD,
-                in1=mask_scaled[:], op0=ALU.mult, op1=ALU.add,
-            )
-            nc.vector.tensor_scalar(
-                out=prior_t[:, h, :], in0=power[:, h, :], scalar1=-ROOT_HD, scalar2=None, op0=ALU.mult
-            )
+
+        def ring_bank(tile_shape, dtype):
+            return ring_psum.tile(tile_shape, dtype, tag="bank", name="ring_bank")
+
+        def prior_distance():
+            nc.scalar.activation(out=exp_loc[:], in_=loc_bf[:], func=ACT.Exp)
+            nc.scalar.activation(out=exp_neg_loc[:], in_=loc_bf[:], func=ACT.Exp, scale=-1.0)
+            nc.scalar.activation(out=slope[:], in_=scale_bf[:], func=ACT.Exp)
+            nc.scalar.activation(out=warm[:], in_=slope[:, 0:1], func=ACT.Ln)
+            nc.vector.tensor_sub(out=offset[:], in0=exp_loc[:], in1=exp_neg_loc[:])
+            nc.vector.tensor_copy(out=shape_f[:], in_=shape_bf[:])
+            for h in range(H):
+                nc.vector.tensor_scalar(
+                    out=z[:, h, :], in0=dist[:], scalar1=offset[:, h : h + 1], scalar2=slope[:, h : h + 1],
+                    op0=ALU.subtract, op1=ALU.mult,
+                )
+            for h in range(H):
+                nc.vector.scalar_tensor_tensor(
+                    out=abs_z[:, h, :], in0=z[:, h, :], scalar=-1.0, in1=z[:, h, :], op0=ALU.mult, op1=ALU.max
+                )
+
+        def prior_power():
+            for h in range(H):
+                nc.scalar.activation(out=log_z[:, h, :], in_=abs_z[:, h, :], func=ACT.Ln, bias=eps_col[:])
+            for h in range(H):
+                nc.scalar.activation(
+                    out=prior_t[:, h, :], in_=log_z[:, h, :], func=ACT.Exp, scale=shape_f[:, h : h + 1],
+                    bias=log_root[:],
+                )
+
+        def turn_mask():
+            bank = score_psum.tile([P, NT, P], BF16, tag="bank", name="mask_bank")
+            for t in range(NT):
+                nc.tensor.transpose(bank[:, t, :], mask_sb[:, t, :], ident_bf[:])
+            return bank
+
+        def prior_diagonal(mask_t):
+            for h in range(H):
+                nc.vector.scalar_tensor_tensor(
+                    out=diag_t[:, h, :, :], in0=mask_t[:], scalar=-ROOT_HD,
+                    in1=prior_t[:, h, :P].unsqueeze(1).to_broadcast([P, NT, P]), op0=ALU.mult, op1=ALU.add,
+                )
 
         x_grouped, x_codes, x_scales, v_grouped = {}, {}, {}, {}
         q_t, k_t, v_codes, v_scales = {}, {}, {}, {}
 
-        def turn_x(b, half):
-            if half == 0:
+        def copy_out(engine, dst, src):
+            if engine == "V":
+                nc.vector.tensor_copy(out=dst, in_=src)
+            else:
+                nc.scalar.copy(out=dst, in_=src)
+
+        def turn_k(b, h):
+            if h == 0:
+                k_t[b] = batch.tile([P, H, NT, P], BF16, name="k_t")
+            bank = ring_bank([P, NT, P], BF16)
+            for pos in range(NT):
+                t = KEY_TILE[b % TWIN][pos]
+                nc.tensor.matmul(
+                    out=bank[:, pos, :], lhsT=k_sb[b][:, t, h * HD : (h + 1) * HD], rhs=ident_bf[:], start=True, stop=True
+                )
+            return k_t[b][:, h, :, :], bank[:]
+
+        def turn_q(b, h):
+            if h == 0:
+                q_t[b] = batch.tile([P, H, NT, P], BF16, name="q_t")
+            bank = ring_bank([P, NT, P], BF16)
+            for t in range(NT):
+                nc.tensor.matmul(
+                    out=bank[:, t, :], lhsT=q_sb[b][:, t, h * HD : (h + 1) * HD], rhs=minus_ident_bf[:],
+                    start=True, stop=True,
+                )
+            return q_t[b][:, h, :, :], bank[:]
+
+        def turn_x(b, u):
+            if u == 0:
                 x_grouped[b] = batch.tile([P, PACK, P, PACK], BF16, name="x_grouped", align_bytes=64)
             x_words = x_sb[b][:].bitcast(F32)
             grouped_words = (
                 x_grouped[b][:].rearrange("p t r c -> p (t r c)").bitcast(F32).rearrange("p (t r f) -> p t r f", t=PACK, f=2)
             )
-            x_ps = prep_psum.tile([P, 2, 2, P], F32, tag="prep")
-            for tt in range(2):
+            bank = ring_bank([P, 2, 2, P], F32)
+            for e in range(2):
                 for f in range(2):
-                    nc.tensor.transpose(x_ps[:, tt, f, :], x_words[:, 2 * half + tt, f : D // 2 : 2], ident_f32[:])
-            nc.vector.tensor_copy(
-                out=grouped_words[:, 2 * half : 2 * half + 2, :, :], in_=x_ps[:].rearrange("p t f r -> p t r f")
-            )
+                    nc.tensor.transpose(bank[:, e, f, :], x_words[:, 2 * u + e, f : D // 2 : 2], ident_f32[:])
+            return grouped_words[:, 2 * u : 2 * u + 2, :, :], bank[:].rearrange("p t f r -> p t r f")
 
         def quantise_x(b):
             x_codes[b] = batch.tile([P, PACK * P], U32, name="x_codes", align_bytes=64)
@@ -158,29 +226,13 @@ def tile_bayesianattention_pa_t_kernel(tc, x, wv_words, wv_scales, q, k, mask, s
                 in_=x_grouped[b][:].rearrange("p t r c -> p (t r c)"),
             )
 
-        def turn_rows(b, piece):
-            name, rows, turned = ("q_t", q_sb[b], q_t) if piece < H else ("k_t", k_sb[b], k_t)
-            h = piece % H
-            if h == 0:
-                turned[b] = batch.tile([P, H, S], BF16, name=name)
-            t_ps = prep_psum.tile([P, S], BF16, tag="prep")
-            for t in range(NT):
-                nc.tensor.matmul(
-                    out=t_ps[:, t * P : (t + 1) * P], lhsT=rows[:, t, h * HD : (h + 1) * HD], rhs=ident_bf[:],
-                    start=True, stop=True,
-                )
-            if piece < 2 * H - 1:
-                nc.scalar.copy(out=turned[b][:, h, :], in_=t_ps[:])
-            else:
-                nc.vector.tensor_copy(out=turned[b][:, h, :], in_=t_ps[:])
-
         def project_v(b, h):
             if h == 0:
                 v_grouped[b] = batch.tile([P, H, HD, PACK], BF16, name="v_grouped", align_bytes=64)
-            v_ps = prep_psum.tile([P, PACK, HD], F32, tag="prep")
+            bank = ring_bank([P, PACK, HD], F32)
             for t in range(PACK):
                 nc.tensor.matmul_mx(
-                    out=v_ps[:, t, :],
+                    out=bank[:, t, :],
                     lhsT=x_codes[b][:, t * P : (t + 1) * P].bitcast(FP8X4),
                     lhsT_scale=x_scales[b][:, t * P : (t + 1) * P],
                     rhs=w_codes[:, h * HD : (h + 1) * HD].bitcast(FP8X4),
@@ -188,135 +240,260 @@ def tile_bayesianattention_pa_t_kernel(tc, x, wv_words, wv_scales, q, k, mask, s
                     start=True,
                     stop=True,
                 )
-            nc.scalar.copy(out=v_grouped[b][:, h, :, :], in_=v_ps[:].rearrange("p t d -> p d t"))
+            return v_grouped[b][:, h, :, :], bank[:].rearrange("p t d -> p d t")
 
-        def quantise_v(b):
-            v_codes[b] = batch.tile([P, E], U32, name="v_codes", align_bytes=64)
-            v_scales[b] = batch.tile([P, E], U8, name="v_scales", align_bytes=64)
+        def quantise_v(b, h):
+            twin, j = divmod(b, TWIN)
+            if h == 0 and j == 0:
+                v_codes[twin] = twins.tile([P, H, TWIN, HD], U32, name="v_codes", align_bytes=64)
+                v_scales[twin] = twins.tile([P, H, TWIN, HD], U8, name="v_scales", align_bytes=64)
             nc.vector.quantize_mx(
-                out=v_codes[b][:].bitcast(FP8X4), scales=v_scales[b][:],
-                in_=v_grouped[b][:].rearrange("p h d t -> p (h d t)"),
+                out=v_codes[twin][:, h, j, :].bitcast(FP8X4), scales=v_scales[twin][:, h, j, :],
+                in_=v_grouped[b][:, h, :, :].rearrange("p d t -> p (d t)"),
             )
 
-        def prepare(b, step):
-            if step < 2 * H:
-                turn_rows(b, step)
-            if step in (1, 3):
-                turn_x(b, (step - 1) // 2)
-            if step == 4:
-                quantise_x(b)
-            if step in (6, 8):
-                project_v(b, (step - 6) // 2)
-            if step == 9:
-                quantise_v(b)
+        def mask_v(b):
+            twin, j = divmod(b, TWIN)
+            half = slice(j * HALF, (j + 1) * HALF)
+            nc.vector.tensor_copy(
+                out=v_masked[twin % 2][half, :, j, :].bitcast(I32), in_=v_codes[twin][half, :, j, :].bitcast(I32)
+            )
 
-        def prepare_in_round(n):
-            newest, phase = divmod(n + LEAD, GROUPS)
-            for age in (2, 1, 0):
-                if 0 <= newest - age < B:
-                    prepare(newest - age, age * GROUPS + phase)
+        groups = []
+        for twin in range(B // TWIN):
+            groups += [("long", twin, j, h) for j in range(TWIN) for h in range(H)]
+            groups += [("short", twin, None, h) for h in range(H)]
+        row_sum, inv_sum, e_grouped, e_codes, e_scales, o_bank, o_short = {}, {}, {}, {}, {}, {}, {}
 
-        groups = [(b, pair, h) for b in range(B) for h in range(H) for pair in (1, 0)]
-        e_ps = [fixed_psum.tile([P, 2, 2, P], F32, name="e_ps%d" % pair) for pair in range(2)]
-        o_ps = [fixed_psum.tile([P, 2, H, HD], F32, name="o_ps%d" % pair) for pair in range(2)]
-        neg_max, row_sum, inv_sum = {}, {}, {}
-        e_grouped, e_codes, e_scales = {}, {}, {}
+        def score_bank():
+            return score_psum.tile([P, NT, P], F32, tag="bank", name="score_bank")
 
-        for ii in range(2):
-            nc.tensor.transpose(e_ps[0][:, ii, 1, :], e_sb[:, 0, 0, :].bitcast(F32)[:, P : 2 * P], ident_f32[:])
-
-        def scores_and_exp(n):
-            b, pair, h = groups[n]
-            if h == 0:
-                neg_max[b, pair] = stats.tile([P, 2, H], F32, name="neg_max")
-                row_sum[b, pair] = stats.tile([P, 2, H], F32, name="row_sum")
-            for ii in (1, 0):
-                it = 2 * pair + ii
-                keys = (it + 1) * P
-                s_ps = score_psum.tile([P, S], F32)
-                for jt in range(it + 1):
-                    nc.tensor.matmul(
-                        out=s_ps[:, jt * P : (jt + 1) * P],
-                        lhsT=diag_t[:, h, it, :] if jt == it else prior_t[:, h, (it - jt) * P : (it - jt + 1) * P],
-                        rhs=ident_f32[:],
-                        is_transpose=True,
-                        start=(jt == 0),
-                        stop=False,
-                    )
+        def add_scores(bank, b, h, it, positions, columns):
+            for i, pos in enumerate(positions):
+                jt = KEY_TILE[b % TWIN][pos]
                 nc.tensor.matmul(
-                    out=s_ps[:, :keys], lhsT=q_t[b][:, h, it * P : (it + 1) * P], rhs=k_t[b][:, h, :keys],
-                    start=False, stop=True,
+                    out=bank[:, pos, :] if columns is None else bank[:, columns, :],
+                    lhsT=diag_t[:, h, it, :] if jt == it else prior_t[:, h, (it - jt) * P : (it - jt + 1) * P],
+                    rhs=ident_f32[:],
+                    is_transpose=True,
+                    start=(i == 0),
+                    stop=False,
                 )
-                neg_s = work.tile([P, S], F32)
-                nc.vector.tensor_scalar(
-                    out=neg_s[:, :keys], in0=s_ps[:, :keys], scalar1=-1.0 / ROOT_HD, scalar2=None,
-                    op0=ALU.mult, op1=ALU.min, accum_out=neg_max[b, pair][:, ii, h : h + 1],
+            step = positions[1] - positions[0] if len(positions) > 1 else 1
+            span = slice(positions[0], positions[-1] + 1, step)
+            nc.tensor.matmul(
+                out=bank[:, span, :] if columns is None else bank[:, columns, :],
+                lhsT=q_t[b][:, h, it, :], rhs=k_t[b][:, h, span, :], start=False, stop=True,
+            )
+
+        def exp_bias(bank_view, axis):
+            rows = bank_view.shape[1] if axis is not None else 1
+            low = stats.tile([P, rows], F32, name="low")
+            nc.vector.tensor_reduce(out=low[:], in_=bank_view, axis=axis, op=ALU.min)
+            bias = stats.tile([P, rows], F32, name="bias")
+            nc.gpsimd.tensor_scalar(
+                out=bias[:], in0=low[:], scalar1=1.0 / ROOT_HD, scalar2=0.0, op0=ALU.mult, op1=ALU.add
+            )
+            return bias
+
+        def exponential(n, ii):
+            for dst, src, bias, total in pending[n, ii]:
+                nc.scalar.activation(out=dst, in_=src, func=ACT.Exp, scale=-1.0 / ROOT_HD, bias=bias, accum_out=total)
+
+        pending = {}
+
+        def long_tile(n, ii):
+            kind, twin, j, h = groups[n]
+            b = TWIN * twin + j
+            if h == 0 and ii == 1:
+                row_sum[b] = stats.tile([P, 2, H], F32, name="row_sum")
+            it = 2 + ii
+            live = [pos for pos in range(NT) if KEY_TILE[j][pos] <= it]
+            span = slice(live[0], live[-1] + 1)
+            bank = score_bank()
+            add_scores(bank, b, h, it, live, None)
+            bias = exp_bias(bank[:, span, :].rearrange("p (a t) c -> p a (t c)", a=1), AX.X)
+            pending[n, ii] = [
+                (e_long[j, h][:, ii, span, :], bank[:, span, :], bias[:, 0:1], row_sum[b][:, ii, h : h + 1])
+            ]
+
+        def short_tile(n, it):
+            kind, twin, j, h = groups[n]
+            if it == 1:
+                row_sum[twin, h] = stats.tile([P, 2, TWIN], F32, name="row_sum")
+            bank = score_bank()
+            for j in range(TWIN):
+                b = TWIN * twin + j
+                add_scores(bank, b, h, it, [pos for pos in range(NT) if KEY_TILE[j][pos] <= it], None)
+            if it == 1:
+                bias = exp_bias(bank[:].rearrange("p (u j) c -> p j u c", j=TWIN), AX.XY)
+            else:
+                bias = exp_bias(bank[:, 0:TWIN, :], AX.X)
+            pending[n, it] = []
+            for j in range(TWIN):
+                span = slice(j, NT, TWIN) if it == 1 else slice(j, j + 1)
+                pending[n, it].append(
+                    (e_short[h][:, it, span, :], bank[:, span, :], bias[:, j : j + 1], row_sum[twin, h][:, it, j : j + 1])
                 )
-                nc.scalar.activation(
-                    out=e_sb[:, it, h, :keys], in_=neg_s[:, :keys], func=ACT.Exp, scale=-1.0,
-                    bias=neg_max[b, pair][:, ii, h : h + 1], accum_out=row_sum[b, pair][:, ii, h : h + 1],
-                )
+
+        def score_tile(n, ii):
+            if groups[n][0] == "long":
+                long_tile(n, ii)
+            else:
+                short_tile(n, ii)
 
         def turn_e(n):
-            b, pair, h = groups[n]
+            kind, twin, j, h = groups[n]
+            rows = e_long[j, h] if kind == "long" else e_short[h]
+            bank = ring_bank([P, 2, 2, P], F32)
             for ii in range(2):
-                e_words = e_sb[:, 2 * pair + ii, h, :].bitcast(F32)
-                for u in range(pair + 1):
-                    nc.tensor.transpose(e_ps[pair][:, ii, u, :], e_words[:, u * P : (u + 1) * P], ident_f32[:])
+                words = rows[:, ii, :, :].rearrange("p t c -> p (t c)").bitcast(F32)
+                for u in range(2):
+                    nc.tensor.transpose(bank[:, ii, u, :], words[:, u * P : (u + 1) * P], ident_f32[:])
             e_grouped[n] = work.tile([P, 2, P, PACK], BF16, name="e_grouped", align_bytes=64)
             grouped_words = (
                 e_grouped[n][:].rearrange("p t i c -> p (t i c)").bitcast(F32).rearrange("p (t i u) -> p t i u", t=2, u=2)
             )
-            nc.scalar.copy(out=grouped_words, in_=e_ps[pair][:].rearrange("p t u i -> p t i u"))
+            return grouped_words, bank[:].rearrange("p t u i -> p t i u")
 
         def quantise_e(n):
-            b, pair, h = groups[n]
-            e_codes[n] = work.tile([P, 2 * P], U32, name="e_codes", align_bytes=64)
-            e_scales[n] = work.tile([P, 2 * P], U8, name="e_scales", align_bytes=64)
+            e_codes[n] = work.tile([P, 2, P], U32, name="e_codes", align_bytes=64)
+            e_scales[n] = work.tile([P, 2, P], U8, name="e_scales", align_bytes=64)
             nc.vector.quantize_mx(
-                out=e_codes[n][:].bitcast(FP8X4), scales=e_scales[n][:],
+                out=e_codes[n][:].rearrange("p t i -> p (t i)").bitcast(FP8X4),
+                scales=e_scales[n][:].rearrange("p t i -> p (t i)"),
                 in_=e_grouped[n][:].rearrange("p t i c -> p (t i c)"),
             )
-            if h == H - 1:
-                inv_sum[b, pair] = stats.tile([P, 2, H], F32, name="inv_sum")
-                nc.vector.reciprocal(out=inv_sum[b, pair][:], in_=row_sum[b, pair][:])
 
-        def multiply_and_store(n):
-            b, pair, h = groups[n]
+        def multiply(n):
+            kind, twin, j, h = groups[n]
+            if kind == "short":
+                o_bank[n] = o_psum.tile([P, 2, TWIN, HD], F32, tag="bank", name="o_bank")
+                codes = v_masked[twin % 2][:, h, :, :].rearrange("p j d -> p (j d)")
+                scales = v_scales[twin][:, h, :, :].rearrange("p j d -> p (j d)")
+            else:
+                o_bank[n] = o_psum.tile([P, 2, H, HD], F32, tag="bank", name="o_bank") if h == 0 else o_bank[n - 1]
+                codes = v_codes[twin][:, h, j, :]
+                scales = v_scales[twin][:, h, j, :]
             for ii in range(2):
                 nc.tensor.matmul_mx(
-                    out=o_ps[pair][:, ii, h, :],
-                    lhsT=e_codes[n][:, ii * P : (ii + 1) * P].bitcast(FP8X4),
-                    lhsT_scale=e_scales[n][:, ii * P : (ii + 1) * P],
-                    rhs=v_codes[b][:, h * HD : (h + 1) * HD].bitcast(FP8X4),
-                    rhs_scale=v_scales[b][:, h * HD : (h + 1) * HD],
+                    out=o_bank[n][:, ii, :, :].rearrange("p a d -> p (a d)") if kind == "short" else o_bank[n][:, ii, h, :],
+                    lhsT=e_codes[n][:, ii, :].bitcast(FP8X4),
+                    lhsT_scale=e_scales[n][:, ii, :],
+                    rhs=codes.bitcast(FP8X4),
+                    rhs_scale=scales,
                     start=True,
                     stop=True,
                 )
-            if h == H - 1:
-                o_sb = results.tile([P, 2, H, HD], F32)
-                nc.vector.tensor_tensor(
-                    out=o_sb[:], in0=o_ps[pair][:], in1=inv_sum[b, pair][:].unsqueeze(3).to_broadcast([P, 2, H, HD]),
-                    op=ALU.mult,
-                )
-                rows = out[b, 2 * pair * P : (2 * pair + 2) * P, :]
+
+        def divide_and_store(n):
+            kind, twin, j, h = groups[n]
+            key = (twin, h) if kind == "short" else TWIN * twin + j
+            if kind == "long" and h == 0:
+                return
+            inv_sum[n] = stats.tile([P, 2, 2], F32, name="inv_sum")
+            nc.vector.reciprocal(out=inv_sum[n][:], in_=row_sum[key][:])
+            factor = inv_sum[n][:].unsqueeze(3).to_broadcast([P, 2, 2, HD])
+            if kind == "long":
+                o_sb = results.tile([P, 2, H, HD], F32, name="o_sb")
+                nc.vector.tensor_tensor(out=o_sb[:], in0=o_bank[n][:], in1=factor, op=ALU.mult)
                 nc.sync.dma_start(
-                    out=rows.rearrange("(t p) n -> p t n", p=P), in_=o_sb[:].rearrange("p t h d -> p t (h d)")
+                    out=out[key, 2 * P : 4 * P, :].rearrange("(t p) n -> p t n", p=P),
+                    in_=o_sb[:].rearrange("p t h d -> p t (h d)"),
                 )
+                return
+            if h == 0:
+                o_short[twin] = results.tile([P, 2, TWIN, H, HD], F32, name="o_short")
+            nc.vector.tensor_tensor(out=o_short[twin][:, :, :, h, :], in0=o_bank[n][:], in1=factor, op=ALU.mult)
+            if h == H - 1:
+                for j in range(TWIN):
+                    nc.sync.dma_start(
+                        out=out[TWIN * twin + j, 0 : 2 * P, :].rearrange("(t p) n -> p t n", p=P),
+                        in_=o_short[twin][:, :, j, :, :].rearrange("p t h d -> p t (h d)"),
+                    )
 
-        for n in range(-LEAD, 0):
-            prepare_in_round(n)
+        plan = {
+            -6: ((turn_k, 0, 0, "S"), (turn_q, 0, 0, "S"), (turn_x, 0, 0, "V")),
+            -5: ((turn_k, 0, 1, "S"), (turn_q, 0, 1, "S")),
+            -4: ((turn_k, 1, 0, "S"), (turn_q, 1, 0, "S"), (turn_x, 0, 1, "V")),
+            -3: ((turn_k, 1, 1, "S"),),
+            -2: ((turn_x, 1, 0, "V"), (turn_x, 1, 1, "V")),
+            -1: ((turn_q, 1, 1, "S"), (project_v, 0, 0, "S"), (project_v, 0, 1, "S")),
+            3: ((project_v, 1, 0, "S"), (project_v, 1, 1, "S")),
+        }
+        quantise_plan = {
+            -3: ((quantise_x, 0),), -1: ((quantise_x, 1),), 0: ((quantise_v, 0, 0), (quantise_v, 0, 1)),
+            4: ((quantise_v, 1, 0), (quantise_v, 1, 1)), 5: ((mask_v, 0), (mask_v, 1)),
+        }
 
-        with tc.manual_schedule():
-            for n in range(len(groups) + 5):
-                if n < len(groups):
-                    scores_and_exp(n)
-                if 0 <= n - 3 < len(groups):
-                    quantise_e(n - 3)
-                if n % 2 == 1:
-                    for m in (n - 5, n - 4):
-                        if 0 <= m < len(groups):
-                            multiply_and_store(m)
-                prepare_in_round(n)
-                if 0 <= n - 1 < len(groups):
-                    turn_e(n - 1)
+        def round_step(n, twin):
+            if twin == 0 and n >= -2:
+                return (n - 2 if n < 3 else n) if n >= 0 else None
+            return n - GROUPS * twin
+
+        def pieces(n):
+            return [
+                (step[0], TWIN * twin + step[1], step[2], step[3])
+                for twin in range(B // TWIN)
+                for step in plan.get(round_step(n, twin), ())
+            ]
+
+        def quantise_pieces(n):
+            for twin in range(B // TWIN):
+                for step in quantise_plan.get(round_step(n, twin), ()):
+                    step[0](TWIN * twin + step[1], *step[2:])
+
+        def run_piece(piece):
+            function, b, part, engine = piece
+            return (engine,) + function(b, part)
+
+        prior_distance()
+        prior_power()
+        for n, engines in ((-6, "VVV"), (-5, "VV"), (-4, "SSV"), (-3, "SS")):
+            for piece, engine in zip(pieces(n), engines):
+                copy_out(engine, *run_piece(piece)[1:])
+            if n == -6:
+                mask_t = turn_mask()
+        quantise_x(0)
+        prior_diagonal(mask_t)
+
+        def if_group(step, n, *args):
+            if 0 <= n < len(groups):
+                return step(n, *args)
+
+        for n in range(len(groups) + 6):
+            todo = pieces(n)
+            mx_pieces = [piece for piece in todo if piece[0] == project_v]
+            todo = [piece for piece in todo if piece[0] != project_v]
+            if_group(score_tile, n, 1)
+            first = [run_piece(piece) for piece in todo[:1]]
+            if_group(quantise_e, n - 3)
+            if_group(score_tile, n, 0)
+            if n % 2 == 1:
+                if_group(multiply, n - 5)
+                if_group(multiply, n - 4)
+            second = []
+            for piece in mx_pieces + todo[1:2]:
+                if len(first) + len(second) == RING:
+                    oldest, rest = (first + second)[0], (first + second)[1:]
+                    copy_out(*oldest)
+                    first, second = [], rest
+                second.append(run_piece(piece))
+            for piece in first:
+                copy_out(*piece)
+            if len(second) == RING:
+                copy_out(*second[0])
+                second = second[1:]
+            turned = if_group(turn_e, n - 1)
+            if_group(exponential, n, 1)
+            for piece in second:
+                copy_out(*piece)
+            if_group(exponential, n, 0)
+            if turned:
+                copy_out("S", *turned)
+            quantise_pieces(n)
+            if n % 2 == 1:
+                if_group(divide_and_store, n - 5)
+                if_group(divide_and_store, n - 4)
+            for piece in todo[2:]:
+                copy_out(*run_piece(piece))

@@ -23,7 +23,7 @@ PACK = 4
 EPS = 1e-5
 ROOT_HD = HD**0.5
 TWIN = 2
-RING = 3
+RING = 4
 GROUPS = 6
 LEAD = 6
 
@@ -42,8 +42,8 @@ def tile_bayesianattention_pa_t_kernel(tc, x, wv_words, wv_scales, q, k, mask, s
         work = ctx.enter_context(tc.tile_pool(name="work", bufs=5))
         stats = ctx.enter_context(tc.tile_pool(name="stats", bufs=8))
         results = ctx.enter_context(tc.tile_pool(name="results", bufs=3))
-        score_psum = ctx.enter_context(tc.psum_pool(name="score_psum", bufs=3))
-        ring_psum = ctx.enter_context(tc.psum_pool(name="ring_psum", bufs=3))
+        score_psum = ctx.enter_context(tc.psum_pool(name="score_psum", bufs=2))
+        ring_psum = ctx.enter_context(tc.psum_pool(name="ring_psum", bufs=4))
         o_psum = ctx.enter_context(tc.psum_pool(name="o_psum", bufs=2))
         ctx.enter_context(tc.manual_schedule())
 
@@ -167,12 +167,11 @@ def tile_bayesianattention_pa_t_kernel(tc, x, wv_words, wv_scales, q, k, mask, s
                 nc.tensor.transpose(bank[:, t, :], mask_sb[:, t, :], ident_bf[:])
             return bank
 
-        def prior_diagonal(mask_t):
-            for h in range(H):
-                nc.vector.scalar_tensor_tensor(
-                    out=diag_t[:, h, :, :], in0=mask_t[:], scalar=-ROOT_HD,
-                    in1=prior_t[:, h, :P].unsqueeze(1).to_broadcast([P, NT, P]), op0=ALU.mult, op1=ALU.add,
-                )
+        def prior_diagonal(h, mask_t):
+            nc.vector.scalar_tensor_tensor(
+                out=diag_t[:, h, :, :], in0=mask_t[:], scalar=-ROOT_HD,
+                in1=prior_t[:, h, :P].unsqueeze(1).to_broadcast([P, NT, P]), op0=ALU.mult, op1=ALU.add,
+            )
 
         x_grouped, x_codes, x_scales, v_grouped = {}, {}, {}, {}
         q_t, k_t, v_codes, v_scales = {}, {}, {}, {}
@@ -286,19 +285,14 @@ def tile_bayesianattention_pa_t_kernel(tc, x, wv_words, wv_scales, q, k, mask, s
                 lhsT=q_t[b][:, h, it, :], rhs=k_t[b][:, h, span, :], start=False, stop=True,
             )
 
-        def exp_bias(bank_view, axis):
-            rows = bank_view.shape[1] if axis is not None else 1
-            low = stats.tile([P, rows], F32, name="low")
-            nc.vector.tensor_reduce(out=low[:], in_=bank_view, axis=axis, op=ALU.min)
-            bias = stats.tile([P, rows], F32, name="bias")
-            nc.gpsimd.tensor_scalar(
-                out=bias[:], in0=low[:], scalar1=1.0 / ROOT_HD, scalar2=0.0, op0=ALU.mult, op1=ALU.add
+        def negate(neg, bank_view, low):
+            nc.vector.tensor_scalar(
+                out=neg, in0=bank_view, scalar1=1.0 / ROOT_HD, scalar2=None, op0=ALU.mult, op1=ALU.min, accum_out=low
             )
-            return bias
 
         def exponential(n, ii):
             for dst, src, bias, total in pending[n, ii]:
-                nc.scalar.activation(out=dst, in_=src, func=ACT.Exp, scale=-1.0 / ROOT_HD, bias=bias, accum_out=total)
+                nc.scalar.activation(out=dst, in_=src, func=ACT.Exp, scale=-1.0, bias=bias, accum_out=total)
 
         pending = {}
 
@@ -312,9 +306,11 @@ def tile_bayesianattention_pa_t_kernel(tc, x, wv_words, wv_scales, q, k, mask, s
             span = slice(live[0], live[-1] + 1)
             bank = score_bank()
             add_scores(bank, b, h, it, live, None)
-            bias = exp_bias(bank[:, span, :].rearrange("p (a t) c -> p a (t c)", a=1), AX.X)
+            neg_s = work.tile([P, NT, P], F32, name="neg_s")
+            low = stats.tile([P, TWIN], F32, name="low")
+            negate(neg_s[:, span, :], bank[:, span, :], low[:, 0:1])
             pending[n, ii] = [
-                (e_long[j, h][:, ii, span, :], bank[:, span, :], bias[:, 0:1], row_sum[b][:, ii, h : h + 1])
+                (e_long[j, h][:, ii, span, :], neg_s[:, span, :], low[:, 0:1], row_sum[b][:, ii, h : h + 1])
             ]
 
         def short_tile(n, it):
@@ -325,15 +321,14 @@ def tile_bayesianattention_pa_t_kernel(tc, x, wv_words, wv_scales, q, k, mask, s
             for j in range(TWIN):
                 b = TWIN * twin + j
                 add_scores(bank, b, h, it, [pos for pos in range(NT) if KEY_TILE[j][pos] <= it], None)
-            if it == 1:
-                bias = exp_bias(bank[:].rearrange("p (u j) c -> p j u c", j=TWIN), AX.XY)
-            else:
-                bias = exp_bias(bank[:, 0:TWIN, :], AX.X)
+            neg_s = work.tile([P, NT, P], F32, name="neg_s")
+            low = stats.tile([P, TWIN], F32, name="low")
             pending[n, it] = []
             for j in range(TWIN):
                 span = slice(j, NT, TWIN) if it == 1 else slice(j, j + 1)
+                negate(neg_s[:, span, :], bank[:, span, :], low[:, j : j + 1])
                 pending[n, it].append(
-                    (e_short[h][:, it, span, :], bank[:, span, :], bias[:, j : j + 1], row_sum[twin, h][:, it, j : j + 1])
+                    (e_short[h][:, it, span, :], neg_s[:, span, :], low[:, j : j + 1], row_sum[twin, h][:, it, j : j + 1])
                 )
 
         def score_tile(n, ii):
@@ -413,87 +408,97 @@ def tile_bayesianattention_pa_t_kernel(tc, x, wv_words, wv_scales, q, k, mask, s
                     )
 
         plan = {
-            -6: ((turn_k, 0, 0, "S"), (turn_q, 0, 0, "S"), (turn_x, 0, 0, "V")),
-            -5: ((turn_k, 0, 1, "S"), (turn_q, 0, 1, "S")),
-            -4: ((turn_k, 1, 0, "S"), (turn_q, 1, 0, "S"), (turn_x, 0, 1, "V")),
-            -3: ((turn_k, 1, 1, "S"),),
-            -2: ((turn_x, 1, 0, "V"), (turn_x, 1, 1, "V")),
-            -1: ((turn_q, 1, 1, "S"), (project_v, 0, 0, "S"), (project_v, 0, 1, "S")),
-            3: ((project_v, 1, 0, "S"), (project_v, 1, 1, "S")),
+            -6: ((turn_k, 0, 0, "S"), (turn_q, 0, 0, "S"), None),
+            -5: ((turn_k, 0, 1, "S"), None, (turn_x, 0, 0, "V")),
+            -4: ((turn_q, 0, 1, "S"), (turn_k, 1, 0, "S"), None),
+            -3: (None, None, (turn_x, 0, 1, "S")),
+            -2: ((turn_q, 1, 0, "S"), (turn_k, 1, 1, "S"), None),
+            -1: ((turn_q, 1, 1, "S"), None, None),
+            0: (None, None, (turn_x, 1, 0, "V")),
+            2: (None, None, (turn_x, 1, 1, "S")),
         }
+        project_plan = {-1: 0, 3: 1}
         quantise_plan = {
-            -3: ((quantise_x, 0),), -1: ((quantise_x, 1),), 0: ((quantise_v, 0, 0), (quantise_v, 0, 1)),
+            -3: ((quantise_x, 0),), 1: ((quantise_v, 0, 0), (quantise_v, 0, 1)), 2: ((quantise_x, 1),),
             4: ((quantise_v, 1, 0), (quantise_v, 1, 1)), 5: ((mask_v, 0), (mask_v, 1)),
         }
 
-        def round_step(n, twin):
-            if twin == 0 and n >= -2:
-                return (n - 2 if n < 3 else n) if n >= 0 else None
-            return n - GROUPS * twin
+        waiting = []
 
-        def pieces(n):
-            return [
-                (step[0], TWIN * twin + step[1], step[2], step[3])
-                for twin in range(B // TWIN)
-                for step in plan.get(round_step(n, twin), ())
-            ]
+        def empty(count):
+            for ready in waiting[:count]:
+                copy_out(*ready)
+            waiting[:count] = []
 
-        def quantise_pieces(n):
-            for twin in range(B // TWIN):
-                for step in quantise_plan.get(round_step(n, twin), ()):
-                    step[0](TWIN * twin + step[1], *step[2:])
+        def fill(engine, function, *args):
+            if len(waiting) == RING:
+                empty(1)
+            waiting.append((engine,) + function(*args))
 
-        def run_piece(piece):
-            function, b, part, engine = piece
-            return (engine,) + function(b, part)
+        def twin_steps(n):
+            steps = [(twin, n - GROUPS * twin) for twin in range(B // TWIN)]
+            return ([(0, -1)] if n == 0 else []) + steps
 
-        prior_distance()
-        prior_power()
-        for n, engines in ((-6, "VVV"), (-5, "VV"), (-4, "SSV"), (-3, "SS")):
-            for piece, engine in zip(pieces(n), engines):
-                copy_out(engine, *run_piece(piece)[1:])
-            if n == -6:
-                mask_t = turn_mask()
-        quantise_x(0)
-        prior_diagonal(mask_t)
+        done = []
+
+        def turn_piece(twin, step, place, engine=None):
+            piece = plan.get(step, (None, None, None))[place]
+            if piece is not None and (twin, piece) not in done:
+                done.append((twin, piece))
+                fill(engine or piece[3], piece[0], TWIN * twin + piece[1], piece[2])
+
+        def turn(n, place):
+            for twin, step in twin_steps(n):
+                turn_piece(twin, step, place)
+
+        def project(n):
+            for twin, step in twin_steps(n):
+                if step in project_plan:
+                    for h in range(H):
+                        fill("S", project_v, TWIN * twin + project_plan[step], h)
+
+        def quantise(n):
+            for twin, step in twin_steps(n):
+                for piece in quantise_plan.get(step, ()):
+                    piece[0](TWIN * twin + piece[1], *piece[2:])
 
         def if_group(step, n, *args):
             if 0 <= n < len(groups):
-                return step(n, *args)
+                step(n, *args)
+
+        prior_distance()
+        prior_power()
+        for step, places in ((-6, (0, 1)), (-5, (0, 2)), (-4, (0, 1)), (-2, (0, 1)), (-1, (0,))):
+            for place in places:
+                turn_piece(0, step, place, "V")
+                empty(1)
+            if step == -6:
+                mask_t = turn_mask()
+        prior_diagonal(0, mask_t)
+        turn_piece(0, -3, 2, "V")
+        empty(1)
+        prior_diagonal(1, mask_t)
+        quantise_x(0)
 
         for n in range(len(groups) + 6):
-            todo = pieces(n)
-            mx_pieces = [piece for piece in todo if piece[0] == project_v]
-            todo = [piece for piece in todo if piece[0] != project_v]
             if_group(score_tile, n, 1)
-            first = [run_piece(piece) for piece in todo[:1]]
+            turn(n, 0)
             if_group(quantise_e, n - 3)
             if_group(score_tile, n, 0)
+            turn(n, 2)
             if n % 2 == 1:
                 if_group(multiply, n - 5)
                 if_group(multiply, n - 4)
-            second = []
-            for piece in mx_pieces + todo[1:2]:
-                if len(first) + len(second) == RING:
-                    oldest, rest = (first + second)[0], (first + second)[1:]
-                    copy_out(*oldest)
-                    first, second = [], rest
-                second.append(run_piece(piece))
-            for piece in first:
-                copy_out(*piece)
-            if len(second) == RING:
-                copy_out(*second[0])
-                second = second[1:]
-            turned = if_group(turn_e, n - 1)
+            project(n)
+            turn(n, 1)
+            empty(1)
+            if 0 <= n - 1 < len(groups):
+                fill("S", turn_e, n - 1)
             if_group(exponential, n, 1)
-            for piece in second:
-                copy_out(*piece)
+            empty(len(waiting) - 1)
             if_group(exponential, n, 0)
-            if turned:
-                copy_out("S", *turned)
-            quantise_pieces(n)
+            empty(len(waiting))
+            quantise(n)
             if n % 2 == 1:
                 if_group(divide_and_store, n - 5)
                 if_group(divide_and_store, n - 4)
-            for piece in todo[2:]:
-                copy_out(*run_piece(piece))

@@ -25,7 +25,6 @@ ROOT_HD = HD**0.5
 TWIN = 2
 RING = 4
 GROUPS = 6
-LEAD = 6
 
 KEY_TILE = ((0, 2, 1, 3), (3, 0, 2, 1))
 
@@ -182,27 +181,32 @@ def tile_bayesianattention_pa_t_kernel(tc, x, wv_words, wv_scales, q, k, mask, s
             else:
                 nc.scalar.copy(out=dst, in_=src)
 
-        def turn_k(b, h):
-            if h == 0:
-                k_t[b] = batch.tile([P, H, NT, P], BF16, name="k_t")
-            bank = ring_bank([P, NT, P], BF16)
-            for pos in range(NT):
-                t = KEY_TILE[b % TWIN][pos]
-                nc.tensor.matmul(
-                    out=bank[:, pos, :], lhsT=k_sb[b][:, t, h * HD : (h + 1) * HD], rhs=ident_bf[:], start=True, stop=True
-                )
-            return k_t[b][:, h, :, :], bank[:]
+        def turn_rows(rows, turned, tiles, identity, heads):
+            if 0 in heads:
+                half_full.append(ring_bank([P, H, NT, P], BF16))
+            bank = half_full[0]
+            for h in heads:
+                for pos in range(NT):
+                    nc.tensor.matmul(
+                        out=bank[:, h, pos, :], lhsT=rows[:, tiles[pos], h * HD : (h + 1) * HD], rhs=identity[:],
+                        start=True, stop=True,
+                    )
+            if H - 1 not in heads:
+                return None
+            half_full.clear()
+            return turned[:], bank[:]
 
-        def turn_q(b, h):
-            if h == 0:
+        half_full = []
+
+        def turn_k(b, heads):
+            if 0 in heads:
+                k_t[b] = batch.tile([P, H, NT, P], BF16, name="k_t")
+            return turn_rows(k_sb[b], k_t[b], KEY_TILE[b % TWIN], ident_bf, heads)
+
+        def turn_q(b, heads):
+            if 0 in heads:
                 q_t[b] = batch.tile([P, H, NT, P], BF16, name="q_t")
-            bank = ring_bank([P, NT, P], BF16)
-            for t in range(NT):
-                nc.tensor.matmul(
-                    out=bank[:, t, :], lhsT=q_sb[b][:, t, h * HD : (h + 1) * HD], rhs=minus_ident_bf[:],
-                    start=True, stop=True,
-                )
-            return q_t[b][:, h, :, :], bank[:]
+            return turn_rows(q_sb[b], q_t[b], range(NT), minus_ident_bf, heads)
 
         def turn_x(b, u):
             if u == 0:
@@ -226,8 +230,9 @@ def tile_bayesianattention_pa_t_kernel(tc, x, wv_words, wv_scales, q, k, mask, s
             )
 
         def project_v(b, h):
-            if h == 0:
-                v_grouped[b] = batch.tile([P, H, HD, PACK], BF16, name="v_grouped", align_bytes=64)
+            twin, j = divmod(b, TWIN)
+            if h == 0 and j == 0:
+                v_grouped[twin] = twins.tile([P, H, TWIN, HD, PACK], BF16, name="v_grouped", align_bytes=64)
             bank = ring_bank([P, PACK, HD], F32)
             for t in range(PACK):
                 nc.tensor.matmul_mx(
@@ -239,24 +244,25 @@ def tile_bayesianattention_pa_t_kernel(tc, x, wv_words, wv_scales, q, k, mask, s
                     start=True,
                     stop=True,
                 )
-            return v_grouped[b][:, h, :, :], bank[:].rearrange("p t d -> p d t")
+            return v_grouped[twin][:, h, j, :, :], bank[:].rearrange("p t d -> p d t")
 
-        def quantise_v(b, h):
-            twin, j = divmod(b, TWIN)
-            if h == 0 and j == 0:
-                v_codes[twin] = twins.tile([P, H, TWIN, HD], U32, name="v_codes", align_bytes=64)
-                v_scales[twin] = twins.tile([P, H, TWIN, HD], U8, name="v_scales", align_bytes=64)
+        def quantise_v(b):
+            twin = b // TWIN
+            v_codes[twin] = twins.tile([P, H, TWIN, HD], U32, name="v_codes", align_bytes=64)
+            v_scales[twin] = twins.tile([P, H, TWIN, HD], U8, name="v_scales", align_bytes=64)
             nc.vector.quantize_mx(
-                out=v_codes[twin][:, h, j, :].bitcast(FP8X4), scales=v_scales[twin][:, h, j, :],
-                in_=v_grouped[b][:, h, :, :].rearrange("p d t -> p (d t)"),
+                out=v_codes[twin][:].rearrange("p h j d -> p (h j d)").bitcast(FP8X4),
+                scales=v_scales[twin][:].rearrange("p h j d -> p (h j d)"),
+                in_=v_grouped[twin][:].rearrange("p h j d t -> p (h j d t)"),
             )
 
         def mask_v(b):
-            twin, j = divmod(b, TWIN)
-            half = slice(j * HALF, (j + 1) * HALF)
-            nc.vector.tensor_copy(
-                out=v_masked[twin % 2][half, :, j, :].bitcast(I32), in_=v_codes[twin][half, :, j, :].bitcast(I32)
-            )
+            twin = b // TWIN
+            for j in range(TWIN):
+                half = slice(j * HALF, (j + 1) * HALF)
+                nc.sync.dma_start(
+                    out=v_masked[twin % 2][half, :, j, :].bitcast(I32), in_=v_codes[twin][half, :, j, :].bitcast(I32)
+                )
 
         groups = []
         for twin in range(B // TWIN):
@@ -299,8 +305,8 @@ def tile_bayesianattention_pa_t_kernel(tc, x, wv_words, wv_scales, q, k, mask, s
         def long_tile(n, ii):
             kind, twin, j, h = groups[n]
             b = TWIN * twin + j
-            if h == 0 and ii == 1:
-                row_sum[b] = stats.tile([P, 2, H], F32, name="row_sum")
+            if h == 0 and j == 0 and ii == 1:
+                row_sum["long", twin] = stats.tile([P, TWIN, 2, H], F32, name="row_sum")
             it = 2 + ii
             live = [pos for pos in range(NT) if KEY_TILE[j][pos] <= it]
             span = slice(live[0], live[-1] + 1)
@@ -310,13 +316,13 @@ def tile_bayesianattention_pa_t_kernel(tc, x, wv_words, wv_scales, q, k, mask, s
             low = stats.tile([P, TWIN], F32, name="low")
             negate(neg_s[:, span, :], bank[:, span, :], low[:, 0:1])
             pending[n, ii] = [
-                (e_long[j, h][:, ii, span, :], neg_s[:, span, :], low[:, 0:1], row_sum[b][:, ii, h : h + 1])
+                (e_long[j, h][:, ii, span, :], neg_s[:, span, :], low[:, 0:1], row_sum[kind, twin][:, j, ii, h : h + 1])
             ]
 
         def short_tile(n, it):
             kind, twin, j, h = groups[n]
-            if it == 1:
-                row_sum[twin, h] = stats.tile([P, 2, TWIN], F32, name="row_sum")
+            if it == 1 and h == 0:
+                row_sum["short", twin] = stats.tile([P, H, 2, TWIN], F32, name="row_sum")
             bank = score_bank()
             for j in range(TWIN):
                 b = TWIN * twin + j
@@ -328,7 +334,7 @@ def tile_bayesianattention_pa_t_kernel(tc, x, wv_words, wv_scales, q, k, mask, s
                 span = slice(j, NT, TWIN) if it == 1 else slice(j, j + 1)
                 negate(neg_s[:, span, :], bank[:, span, :], low[:, j : j + 1])
                 pending[n, it].append(
-                    (e_short[h][:, it, span, :], neg_s[:, span, :], low[:, j : j + 1], row_sum[twin, h][:, it, j : j + 1])
+                    (e_short[h][:, it, span, :], neg_s[:, span, :], low[:, j : j + 1], row_sum[kind, twin][:, h, it, j : j + 1])
                 )
 
         def score_tile(n, ii):
@@ -381,19 +387,20 @@ def tile_bayesianattention_pa_t_kernel(tc, x, wv_words, wv_scales, q, k, mask, s
                     stop=True,
                 )
 
+        def invert_sums(kind, twin):
+            inv_sum[kind, twin] = stats.tile([P, 2, 2, 2], F32, name="inv_sum")
+            nc.vector.reciprocal(out=inv_sum[kind, twin][:], in_=row_sum[kind, twin][:])
+
         def divide_and_store(n):
             kind, twin, j, h = groups[n]
-            key = (twin, h) if kind == "short" else TWIN * twin + j
             if kind == "long" and h == 0:
                 return
-            inv_sum[n] = stats.tile([P, 2, 2], F32, name="inv_sum")
-            nc.vector.reciprocal(out=inv_sum[n][:], in_=row_sum[key][:])
-            factor = inv_sum[n][:].unsqueeze(3).to_broadcast([P, 2, 2, HD])
+            factor = inv_sum[kind, twin][:, j if kind == "long" else h, :, :].unsqueeze(3).to_broadcast([P, 2, 2, HD])
             if kind == "long":
                 o_sb = results.tile([P, 2, H, HD], F32, name="o_sb")
                 nc.vector.tensor_tensor(out=o_sb[:], in0=o_bank[n][:], in1=factor, op=ALU.mult)
                 nc.sync.dma_start(
-                    out=out[key, 2 * P : 4 * P, :].rearrange("(t p) n -> p t n", p=P),
+                    out=out[TWIN * twin + j, 2 * P : 4 * P, :].rearrange("(t p) n -> p t n", p=P),
                     in_=o_sb[:].rearrange("p t h d -> p t (h d)"),
                 )
                 return
@@ -401,26 +408,23 @@ def tile_bayesianattention_pa_t_kernel(tc, x, wv_words, wv_scales, q, k, mask, s
                 o_short[twin] = results.tile([P, 2, TWIN, H, HD], F32, name="o_short")
             nc.vector.tensor_tensor(out=o_short[twin][:, :, :, h, :], in0=o_bank[n][:], in1=factor, op=ALU.mult)
             if h == H - 1:
-                for j in range(TWIN):
+                for jj in range(TWIN):
                     nc.sync.dma_start(
-                        out=out[TWIN * twin + j, 0 : 2 * P, :].rearrange("(t p) n -> p t n", p=P),
-                        in_=o_short[twin][:, :, j, :, :].rearrange("p t h d -> p t (h d)"),
+                        out=out[TWIN * twin + jj, 0 : 2 * P, :].rearrange("(t p) n -> p t n", p=P),
+                        in_=o_short[twin][:, :, jj, :, :].rearrange("p t h d -> p t (h d)"),
                     )
 
+        both = (0, 1)
         plan = {
-            -6: ((turn_k, 0, 0, "S"), (turn_q, 0, 0, "S"), None),
-            -5: ((turn_k, 0, 1, "S"), None, (turn_x, 0, 0, "V")),
-            -4: ((turn_q, 0, 1, "S"), (turn_k, 1, 0, "S"), None),
-            -3: (None, None, (turn_x, 0, 1, "S")),
-            -2: ((turn_q, 1, 0, "S"), (turn_k, 1, 1, "S"), None),
-            -1: ((turn_q, 1, 1, "S"), None, None),
-            0: (None, None, (turn_x, 1, 0, "V")),
-            2: (None, None, (turn_x, 1, 1, "S")),
+            -6: ((turn_k, 0, (0,), "S"), (turn_k, 0, (1,), "S"), (turn_x, 0, 0, "S")),
+            -5: ((turn_q, 0, (0,), "S"), (turn_q, 0, (1,), "S"), (turn_x, 0, 1, "V")),
+            -3: ((turn_k, 1, (0,), "S"), (turn_k, 1, (1,), "S"), None),
+            -2: ((turn_q, 1, (0,), "S"), (turn_q, 1, (1,), "S"), (turn_x, 1, 0, "V")),
+            -1: (None, None, (turn_x, 1, 1, "V")),
         }
-        project_plan = {-1: 0, 3: 1}
+        project_plan = {-1: 0, 2: 1}
         quantise_plan = {
-            -3: ((quantise_x, 0),), 1: ((quantise_v, 0, 0), (quantise_v, 0, 1)), 2: ((quantise_x, 1),),
-            4: ((quantise_v, 1, 0), (quantise_v, 1, 1)), 5: ((mask_v, 0), (mask_v, 1)),
+            -4: ((quantise_x, 0),), 0: ((quantise_x, 1),), 3: ((quantise_v, 0), (mask_v, 0)),
         }
 
         waiting = []
@@ -431,36 +435,40 @@ def tile_bayesianattention_pa_t_kernel(tc, x, wv_words, wv_scales, q, k, mask, s
             waiting[:count] = []
 
         def fill(engine, function, *args):
-            if len(waiting) == RING:
+            if len(waiting) + len(half_full) == RING:
                 empty(1)
-            waiting.append((engine,) + function(*args))
+            ready = function(*args)
+            if ready is not None:
+                waiting.append((engine,) + ready)
 
-        def twin_steps(n):
-            steps = [(twin, n - GROUPS * twin) for twin in range(B // TWIN)]
-            return ([(0, -1)] if n == 0 else []) + steps
+        first_plan = {0: (None, None, (turn_x, 1, 0, "V")), 1: (None, None, (turn_x, 1, 1, "S"))}
+        first_project_plan = {0: 0, 2: 1}
+        first_quantise_plan = {1: ((quantise_x, 1),), 3: ((quantise_v, 0), (mask_v, 0))}
 
-        done = []
-
-        def turn_piece(twin, step, place, engine=None):
-            piece = plan.get(step, (None, None, None))[place]
-            if piece is not None and (twin, piece) not in done:
-                done.append((twin, piece))
-                fill(engine or piece[3], piece[0], TWIN * twin + piece[1], piece[2])
+        def planned(n, plan_of_first, plan_of_others):
+            found = []
+            for twin in range(B // TWIN):
+                step = n - GROUPS * twin
+                entry = (plan_of_others if twin else plan_of_first).get(step)
+                if entry is not None:
+                    found.append((TWIN * twin, entry))
+            return found
 
         def turn(n, place):
-            for twin, step in twin_steps(n):
-                turn_piece(twin, step, place)
+            for b, entry in planned(n, first_plan, plan):
+                if entry[place] is not None:
+                    function, j, part, engine = entry[place]
+                    fill(engine, function, b + j, part)
 
         def project(n):
-            for twin, step in twin_steps(n):
-                if step in project_plan:
-                    for h in range(H):
-                        fill("S", project_v, TWIN * twin + project_plan[step], h)
+            for b, j in planned(n, first_project_plan, project_plan):
+                for h in range(H):
+                    fill("S", project_v, b + j, h)
 
         def quantise(n):
-            for twin, step in twin_steps(n):
-                for piece in quantise_plan.get(step, ()):
-                    piece[0](TWIN * twin + piece[1], *piece[2:])
+            for b, entry in planned(n, first_quantise_plan, quantise_plan):
+                for function, j, *rest in entry:
+                    function(b + j, *rest)
 
         def if_group(step, n, *args):
             if 0 <= n < len(groups):
@@ -468,15 +476,12 @@ def tile_bayesianattention_pa_t_kernel(tc, x, wv_words, wv_scales, q, k, mask, s
 
         prior_distance()
         prior_power()
-        for step, places in ((-6, (0, 1)), (-5, (0, 2)), (-4, (0, 1)), (-2, (0, 1)), (-1, (0,))):
-            for place in places:
-                turn_piece(0, step, place, "V")
-                empty(1)
-            if step == -6:
+        for piece in ((turn_k, 0, both), (turn_q, 0, both), (turn_x, 0, 0), (turn_k, 1, both), (turn_q, 1, both)):
+            copy_out("V", *piece[0](*piece[1:]))
+            if piece == (turn_q, 0, both):
                 mask_t = turn_mask()
         prior_diagonal(0, mask_t)
-        turn_piece(0, -3, 2, "V")
-        empty(1)
+        copy_out("V", *turn_x(0, 1))
         prior_diagonal(1, mask_t)
         quantise_x(0)
 
@@ -484,13 +489,14 @@ def tile_bayesianattention_pa_t_kernel(tc, x, wv_words, wv_scales, q, k, mask, s
             if_group(score_tile, n, 1)
             turn(n, 0)
             if_group(quantise_e, n - 3)
+            for kind, delay in (("long", 5), ("short", 8)):
+                if n >= delay and (n - delay) % GROUPS == 0 and (n - delay) // GROUPS < B // TWIN:
+                    invert_sums(kind, (n - delay) // GROUPS)
             if_group(score_tile, n, 0)
-            turn(n, 2)
-            if n % 2 == 1:
-                if_group(multiply, n - 5)
-                if_group(multiply, n - 4)
-            project(n)
             turn(n, 1)
+            if_group(multiply, n - 4)
+            project(n)
+            turn(n, 2)
             empty(1)
             if 0 <= n - 1 < len(groups):
                 fill("S", turn_e, n - 1)
@@ -499,6 +505,4 @@ def tile_bayesianattention_pa_t_kernel(tc, x, wv_words, wv_scales, q, k, mask, s
             if_group(exponential, n, 0)
             empty(len(waiting))
             quantise(n)
-            if n % 2 == 1:
-                if_group(divide_and_store, n - 5)
-                if_group(divide_and_store, n - 4)
+            if_group(divide_and_store, n - 4)

@@ -62,16 +62,10 @@ def tile_bayesianattention_pa_t_kernel(tc, x, wv_words, wv_scales, q, k, mask, s
             q_sb.append(inputs.tile([P, NT, E], BF16, name="q_sb"))
             nc.sync.dma_start(out=q_sb[b][:], in_=q[b].rearrange("(t p) h d -> p t (h d)", p=P))
             x_sb.append(inputs.tile([P, PACK, D], BF16, name="x_sb"))
-            for half in range(2):
-                rows = x_sb[b][half * HALF : (half + 1) * HALF, :, :].rearrange("p (u e) c -> p u (e c)", u=2)
-                tiles = KEY_TILE[b % TWIN][half], KEY_TILE[b % TWIN][half + 2]
-                if tiles[1] == tiles[0] + 1:
-                    src = x[b, tiles[0] * P : (tiles[0] + 2) * P, :].rearrange("(u p e) c -> p u (e c)", u=2, e=2)
-                    nc.sync.dma_start(out=rows, in_=src)
-                else:
-                    for u in range(2):
-                        src = x[b, tiles[u] * P : (tiles[u] + 1) * P, :].rearrange("(p e) c -> p (e c)", e=2)
-                        nc.sync.dma_start(out=rows[:, u, :], in_=src)
+            nc.sync.dma_start(
+                out=x_sb[b][:].rearrange("p (u e) c -> p u (e c)", u=2),
+                in_=x[b].rearrange("(u p e) c -> p u (e c)", u=2, e=2),
+            )
 
         load_batch(0)
         mask_sb = const.tile([P, NT, P], BF16)
@@ -105,6 +99,9 @@ def tile_bayesianattention_pa_t_kernel(tc, x, wv_words, wv_scales, q, k, mask, s
         nc.vector.tensor_scalar(
             out=minus_ident_bf[:], in0=ident_f32[:], scalar1=-1.0, scalar2=None, op0=ALU.mult
         )
+        swapped_f32 = const.tile([P, P], F32)
+        nc.vector.tensor_copy(out=swapped_f32[:, :HALF], in_=ident_f32[:, HALF:])
+        nc.vector.tensor_copy(out=swapped_f32[:, HALF:], in_=ident_f32[:, :HALF])
         dist = const.tile([P, S], F32)
         nc.gpsimd.iota(dist[:], pattern=[[-1, S]], base=0, channel_multiplier=1, allow_small_or_imprecise_dtypes=True)
 
@@ -208,18 +205,23 @@ def tile_bayesianattention_pa_t_kernel(tc, x, wv_words, wv_scales, q, k, mask, s
                 q_t[b] = batch.tile([P, H, NT, P], BF16, name="q_t")
             return turn_rows(q_sb[b], q_t[b], range(NT), minus_ident_bf, heads)
 
-        def turn_x(b, u):
-            if u == 0:
+        def turn_x(b, e):
+            if e == 0:
                 x_grouped[b] = batch.tile([P, PACK, P, PACK], BF16, name="x_grouped", align_bytes=64)
             x_words = x_sb[b][:].bitcast(F32)
             grouped_words = (
                 x_grouped[b][:].rearrange("p t r c -> p (t r c)").bitcast(F32).rearrange("p (t r f) -> p t r f", t=PACK, f=2)
             )
-            bank = ring_bank([P, 2, 2, P], F32)
-            for e in range(2):
+            bank = ring_bank([P, 2, 2, 2, HALF], F32)
+            for u in range(2):
+                place = KEY_TILE[b % TWIN].index(2 * u)
+                identity = ident_f32 if place < 2 else swapped_f32
                 for f in range(2):
-                    nc.tensor.transpose(bank[:, e, f, :], x_words[:, 2 * u + e, f : D // 2 : 2], ident_f32[:])
-            return grouped_words[:, 2 * u : 2 * u + 2, :, :], bank[:].rearrange("p t f r -> p t r f")
+                    nc.tensor.matmul(
+                        out=bank[:, :, f, place % 2, :], lhsT=x_words[:, 2 * u + e, f : D // 2 : 2],
+                        rhs=identity[:].rearrange("p (v r) -> p v r", v=2), is_transpose=True, start=True, stop=True,
+                    )
+            return grouped_words[:, e : PACK : 2, :, :], bank[:].rearrange("p v f h r -> p v (h r) f")
 
         def quantise_x(b):
             x_codes[b] = batch.tile([P, PACK * P], U32, name="x_codes", align_bytes=64)

@@ -51,7 +51,7 @@ def tile_bayesianattention_pa_t_kernel(tc, x, wv_words, wv_scales, q, k, mask, s
         shape_bf = const.tile([P, H], BF16)
         scale_bf = const.tile([P, H], BF16)
         loc_bf = const.tile([P, H], BF16)
-        for dst, src in ((scale_bf, scale), (loc_bf, loc), (shape_bf, shape)):
+        for dst, src in ((loc_bf, loc), (scale_bf, scale), (shape_bf, shape)):
             nc.scalar.dma_start(out=dst[:], in_=src.rearrange("a h b c -> (a h b c)").partition_broadcast(P))
 
         q_sb, k_sb, x_sb = [], [], []
@@ -110,12 +110,12 @@ def tile_bayesianattention_pa_t_kernel(tc, x, wv_words, wv_scales, q, k, mask, s
             for j in range(TWIN):
                 e_long[j, h] = const.tile([P, 2, NT, P], BF16, name="e_long%d%d" % (j, h))
                 dead = KEY_TILE[j].index(NT - 1)
-                nc.vector.memset(e_long[j, h][:, 0, dead, :].bitcast(I32), 0)
+                nc.gpsimd.memset(e_long[j, h][:, 0, dead, :].bitcast(I32), 0)
             e_short.append(const.tile([P, 2, NT, P], BF16, name="e_short%d" % h))
-            nc.vector.memset(e_short[h][:, 0, 2:NT, :].rearrange("p t c -> p (t c)").bitcast(I32), 0)
+            nc.gpsimd.memset(e_short[h][:, 0, 2:NT, :].rearrange("p t c -> p (t c)").bitcast(I32), 0)
         v_masked = [const.tile([P, H, TWIN, HD], U32, name="v_masked%d" % i, align_bytes=64) for i in range(2)]
         for i in range(2):
-            nc.vector.memset(v_masked[i][:].rearrange("p h j d -> p (h j d)").bitcast(I32), 0)
+            nc.gpsimd.memset(v_masked[i][:].rearrange("p h j d -> p (h j d)").bitcast(I32), 0)
 
         slope = const.tile([P, H], F32)
         exp_loc = const.tile([P, H], F32)
@@ -345,40 +345,45 @@ def tile_bayesianattention_pa_t_kernel(tc, x, wv_words, wv_scales, q, k, mask, s
             else:
                 short_tile(n, ii)
 
-        def turn_e(n):
+        def turn_e(n, first=0, count=2):
             kind, twin, j, h = groups[n]
             rows = e_long[j, h] if kind == "long" else e_short[h]
-            bank = ring_bank([P, 2, 2, P], F32)
-            for ii in range(2):
-                words = rows[:, ii, :, :].rearrange("p t c -> p (t c)").bitcast(F32)
+            bank = ring_bank([P, count, 2, P], F32)
+            for i in range(count):
+                words = rows[:, first + i, :, :].rearrange("p t c -> p (t c)").bitcast(F32)
                 for u in range(2):
-                    nc.tensor.transpose(bank[:, ii, u, :], words[:, u * P : (u + 1) * P], ident_f32[:])
-            e_grouped[n] = work.tile([P, 2, P, PACK], BF16, name="e_grouped", align_bytes=64)
+                    nc.tensor.transpose(bank[:, i, u, :], words[:, u * P : (u + 1) * P], ident_f32[:])
+            if n not in e_grouped:
+                e_grouped[n] = work.tile([P, 2, P, PACK], BF16, name="e_grouped", align_bytes=64)
             grouped_words = (
                 e_grouped[n][:].rearrange("p t i c -> p (t i c)").bitcast(F32).rearrange("p (t i u) -> p t i u", t=2, u=2)
             )
-            return grouped_words, bank[:].rearrange("p t u i -> p t i u")
+            return grouped_words[:, first : first + count, :, :], bank[:].rearrange("p t u i -> p t i u")
 
-        def quantise_e(n):
-            e_codes[n] = work.tile([P, 2, P], U32, name="e_codes", align_bytes=64)
-            e_scales[n] = work.tile([P, 2, P], U8, name="e_scales", align_bytes=64)
+        def quantise_e(n, first=0, count=2):
+            if n not in e_codes:
+                e_codes[n] = work.tile([P, 2, P], U32, name="e_codes", align_bytes=64)
+                e_scales[n] = work.tile([P, 2, P], U8, name="e_scales", align_bytes=64)
+            tiles = slice(first, first + count)
             nc.vector.quantize_mx(
-                out=e_codes[n][:].rearrange("p t i -> p (t i)").bitcast(FP8X4),
-                scales=e_scales[n][:].rearrange("p t i -> p (t i)"),
-                in_=e_grouped[n][:].rearrange("p t i c -> p (t i c)"),
+                out=e_codes[n][:, tiles, :].rearrange("p t i -> p (t i)").bitcast(FP8X4),
+                scales=e_scales[n][:, tiles, :].rearrange("p t i -> p (t i)"),
+                in_=e_grouped[n][:, tiles, :, :].rearrange("p t i c -> p (t i c)"),
             )
 
-        def multiply(n):
+        def multiply(n, first=0, count=2):
             kind, twin, j, h = groups[n]
             if kind == "short":
-                o_bank[n] = o_psum.tile([P, 2, TWIN, HD], F32, tag="bank", name="o_bank")
+                if n not in o_bank:
+                    pool = o_psum if n < len(groups) - 1 else score_psum
+                    o_bank[n] = pool.tile([P, 2, TWIN, HD], F32, tag="bank", name="o_bank")
                 codes = v_masked[twin % 2][:, h, :, :].rearrange("p j d -> p (j d)")
                 scales = v_scales[twin][:, h, :, :].rearrange("p j d -> p (j d)")
             else:
                 o_bank[n] = o_psum.tile([P, 2, H, HD], F32, tag="bank", name="o_bank") if h == 0 else o_bank[n - 1]
                 codes = v_codes[twin][:, h, j, :]
                 scales = v_scales[twin][:, h, j, :]
-            for ii in range(2):
+            for ii in range(first, first + count):
                 nc.tensor.matmul_mx(
                     out=o_bank[n][:, ii, :, :].rearrange("p a d -> p (a d)") if kind == "short" else o_bank[n][:, ii, h, :],
                     lhsT=e_codes[n][:, ii, :].bitcast(FP8X4),
@@ -393,14 +398,22 @@ def tile_bayesianattention_pa_t_kernel(tc, x, wv_words, wv_scales, q, k, mask, s
             inv_sum[kind, twin] = stats.tile([P, 2, 2, 2], F32, name="inv_sum")
             nc.vector.reciprocal(out=inv_sum[kind, twin][:], in_=row_sum[kind, twin][:])
 
-        def divide_and_store(n):
+        def divide_and_store(n, first=0, count=2):
             kind, twin, j, h = groups[n]
             if kind == "long" and h == 0:
                 return
             factor = inv_sum[kind, twin][:, j if kind == "long" else h, :, :].unsqueeze(3).to_broadcast([P, 2, 2, HD])
             if kind == "long":
                 o_sb = results.tile([P, 2, H, HD], F32, name="o_sb")
-                nc.vector.tensor_tensor(out=o_sb[:], in0=o_bank[n][:], in1=factor, op=ALU.mult)
+                if n < len(groups) - GROUPS // 2:
+                    nc.vector.tensor_tensor(out=o_sb[:], in0=o_bank[n][:], in1=factor, op=ALU.mult)
+                else:
+                    for ii in range(2):
+                        for head in range(H):
+                            nc.scalar.activation(
+                                out=o_sb[:, ii, head, :], in_=o_bank[n][:, ii, head, :], func=ACT.Copy,
+                                scale=inv_sum[kind, twin][:, j, ii, head : head + 1],
+                            )
                 nc.sync.dma_start(
                     out=out[TWIN * twin + j, 2 * P : 4 * P, :].rearrange("(t p) n -> p t n", p=P),
                     in_=o_sb[:].rearrange("p t h d -> p t (h d)"),
@@ -408,25 +421,29 @@ def tile_bayesianattention_pa_t_kernel(tc, x, wv_words, wv_scales, q, k, mask, s
                 return
             if h == 0:
                 o_short[twin] = results.tile([P, 2, TWIN, H, HD], F32, name="o_short")
-            nc.vector.tensor_tensor(out=o_short[twin][:, :, :, h, :], in0=o_bank[n][:], in1=factor, op=ALU.mult)
+            tiles = slice(first, first + count)
+            nc.vector.tensor_tensor(
+                out=o_short[twin][:, tiles, :, h, :], in0=o_bank[n][:, tiles, :, :], in1=factor[:, tiles, :, :], op=ALU.mult
+            )
             if h == H - 1:
                 for jj in range(TWIN):
                     nc.sync.dma_start(
-                        out=out[TWIN * twin + jj, 0 : 2 * P, :].rearrange("(t p) n -> p t n", p=P),
-                        in_=o_short[twin][:, :, jj, :, :].rearrange("p t h d -> p t (h d)"),
+                        out=out[TWIN * twin + jj, first * P : (first + count) * P, :].rearrange("(t p) n -> p t n", p=P),
+                        in_=o_short[twin][:, tiles, jj, :, :].rearrange("p t h d -> p t (h d)"),
                     )
 
         both = (0, 1)
         plan = {
-            -6: ((turn_k, 0, (0,), "S"), (turn_k, 0, (1,), "S"), (turn_x, 0, 0, "S")),
-            -5: ((turn_q, 0, (0,), "S"), (turn_q, 0, (1,), "S"), (turn_x, 0, 1, "V")),
-            -3: ((turn_k, 1, (0,), "S"), (turn_k, 1, (1,), "S"), None),
+            -6: ((turn_k, 0, (0,), "S"), (turn_k, 0, (1,), "S"), None),
+            -5: ((turn_q, 0, (0,), "S"), (turn_q, 0, (1,), "S"), None),
+            -4: (None, None, (turn_x, 0, 0, "V")),
+            -3: ((turn_k, 1, (0,), "S"), (turn_k, 1, (1,), "S"), (turn_x, 0, 1, "S")),
             -2: ((turn_q, 1, (0,), "S"), (turn_q, 1, (1,), "S"), (turn_x, 1, 0, "V")),
             -1: (None, None, (turn_x, 1, 1, "V")),
         }
         project_plan = {-1: 0, 2: 1}
         quantise_plan = {
-            -4: ((quantise_x, 0),), 0: ((quantise_x, 1),), 3: ((quantise_v, 0), (mask_v, 0)),
+            -2: ((quantise_x, 0),), 0: ((quantise_x, 1),), 3: ((quantise_v, 0), (mask_v, 0)),
         }
 
         waiting = []
@@ -460,7 +477,7 @@ def tile_bayesianattention_pa_t_kernel(tc, x, wv_words, wv_scales, q, k, mask, s
             for b, entry in planned(n, first_plan, plan):
                 if entry[place] is not None:
                     function, j, part, engine = entry[place]
-                    fill(engine, function, b + j, part)
+                    fill("V" if n < 1 else engine, function, b + j, part)
 
         def project(n):
             for b, j in planned(n, first_project_plan, project_plan):
@@ -478,16 +495,18 @@ def tile_bayesianattention_pa_t_kernel(tc, x, wv_words, wv_scales, q, k, mask, s
 
         prior_distance()
         prior_power()
-        for piece in ((turn_k, 0, both), (turn_q, 0, both), (turn_x, 0, 0), (turn_k, 1, both), (turn_q, 1, both)):
-            copy_out("V", *piece[0](*piece[1:]))
-            if piece == (turn_q, 0, both):
-                mask_t = turn_mask()
-        prior_diagonal(0, mask_t)
+        copy_out("V", *turn_k(0, both))
+        copy_out("V", *turn_q(0, both))
+        mask_t = turn_mask()
+        copy_out("V", *turn_x(0, 0))
         copy_out("V", *turn_x(0, 1))
+        prior_diagonal(0, mask_t)
+        copy_out("S", *turn_k(1, both))
+        copy_out("S", *turn_q(1, both))
         prior_diagonal(1, mask_t)
         quantise_x(0)
 
-        for n in range(len(groups) + 6):
+        for n in range(len(groups)):
             if_group(score_tile, n, 1)
             turn(n, 0)
             if_group(quantise_e, n - 3)
@@ -508,3 +527,22 @@ def tile_bayesianattention_pa_t_kernel(tc, x, wv_words, wv_scales, q, k, mask, s
             empty(len(waiting))
             quantise(n)
             if_group(divide_and_store, n - 4)
+
+        last = len(groups) - 1
+        multiply(last - 3)
+        fill("S", turn_e, last, 1, 1)
+        fill("S", turn_e, last, 0, 1)
+        quantise_e(last - 2)
+        multiply(last - 2)
+        quantise_e(last - 1)
+        invert_sums("short", B // TWIN - 1)
+        empty(2)
+        quantise_e(last, 1, 1)
+        multiply(last - 1)
+        divide_and_store(last - 2)
+        quantise_e(last, 0, 1)
+        multiply(last, 1, 1)
+        divide_and_store(last - 1)
+        multiply(last, 0, 1)
+        divide_and_store(last, 1, 1)
+        divide_and_store(last, 0, 1)

@@ -48,11 +48,12 @@ def tile_bayesianattention_pa_t_kernel(tc, x, wv_words, wv_scales, q, k, mask, s
 
         w_scales = const.tile([P, E], U8, align_bytes=64)
         nc.vector.memset(w_scales[:].bitcast(I32), 0)
-        shape_bf = const.tile([P, H], BF16)
-        scale_bf = const.tile([P, H], BF16)
-        loc_bf = const.tile([P, H], BF16)
-        for dst, src in ((loc_bf, loc), (scale_bf, scale), (shape_bf, shape)):
-            nc.scalar.dma_start(out=dst[:], in_=src.rearrange("a h b c -> (a h b c)").partition_broadcast(P))
+        params = const.tile([P, 3, 16], BF16)
+        nc.vector.memset(params[:].rearrange("p v h -> p (v h)").bitcast(I32), 0)
+        ones_bf = const.tile([P, P], BF16)
+        nc.vector.memset(ones_bf[:], 1.0)
+        for i, src in enumerate((loc, scale, shape)):
+            nc.scalar.dma_start(out=params[0:1, i, 0:H], in_=src.rearrange("a h b c -> (a b c) h"))
 
         q_sb, k_sb, x_sb = [], [], []
 
@@ -132,12 +133,13 @@ def tile_bayesianattention_pa_t_kernel(tc, x, wv_words, wv_scales, q, k, mask, s
             return ring_psum.tile(tile_shape, dtype, tag="bank", name="ring_bank")
 
         def prior_distance():
-            nc.scalar.activation(out=exp_loc[:], in_=loc_bf[:], func=ACT.Exp)
-            nc.scalar.activation(out=exp_neg_loc[:], in_=loc_bf[:], func=ACT.Exp, scale=-1.0)
-            nc.scalar.activation(out=slope[:], in_=scale_bf[:], func=ACT.Exp)
+            spread = score_psum.tile([P, 3, H], F32, tag="bank", name="spread")
+            nc.tensor.matmul(out=spread[:], lhsT=ones_bf[:], rhs=params[:, :, 0:H], start=True, stop=True)
+            nc.scalar.activation(out=exp_loc[:], in_=spread[:, 0, :], func=ACT.Exp)
+            nc.scalar.activation(out=exp_neg_loc[:], in_=spread[:, 0, :], func=ACT.Exp, scale=-1.0)
+            nc.scalar.activation(out=slope[:], in_=spread[:, 1, :], func=ACT.Exp)
             nc.scalar.activation(out=warm[:], in_=slope[:, 0:1], func=ACT.Ln)
             nc.vector.tensor_sub(out=offset[:], in0=exp_loc[:], in1=exp_neg_loc[:])
-            nc.vector.tensor_copy(out=shape_f[:], in_=shape_bf[:])
             for h in range(H):
                 nc.vector.tensor_scalar(
                     out=z[:, h, :], in0=dist[:], scalar1=offset[:, h : h + 1], scalar2=slope[:, h : h + 1],
@@ -147,6 +149,7 @@ def tile_bayesianattention_pa_t_kernel(tc, x, wv_words, wv_scales, q, k, mask, s
                 nc.vector.scalar_tensor_tensor(
                     out=abs_z[:, h, :], in0=z[:, h, :], scalar=-1.0, in1=z[:, h, :], op0=ALU.mult, op1=ALU.max
                 )
+            nc.vector.tensor_copy(out=shape_f[:], in_=spread[:, 2, :])
 
         def prior_power():
             for h in range(H):

@@ -53,7 +53,7 @@ def tile_bayesianattention_pa_t_kernel(tc, x, wv_words, wv_scales, q, k, mask, s
         ones_bf = const.tile([P, P], BF16)
         nc.vector.memset(ones_bf[:], 1.0)
         for i, src in enumerate((loc, scale, shape)):
-            nc.scalar.dma_start(out=params[0:1, i, 0:H], in_=src.rearrange("a h b c -> (a b c) h"))
+            nc.sync.dma_start(out=params[0:1, i, 0:H], in_=src.rearrange("a h b c -> (a b c) h"))
 
         q_sb, k_sb, x_sb = [], [], []
 
@@ -440,7 +440,7 @@ def tile_bayesianattention_pa_t_kernel(tc, x, wv_words, wv_scales, q, k, mask, s
             -6: ((turn_k, 0, (0,), "S"), (turn_k, 0, (1,), "S"), None),
             -5: ((turn_q, 0, (0,), "S"), (turn_q, 0, (1,), "S"), None),
             -4: (None, None, (turn_x, 0, 0, "V")),
-            -3: ((turn_k, 1, (0,), "S"), (turn_k, 1, (1,), "S"), (turn_x, 0, 1, "S")),
+            -3: ((turn_k, 1, (0,), "S"), (turn_k, 1, (1,), "S"), (turn_x, 0, 1, "V")),
             -2: ((turn_q, 1, (0,), "S"), (turn_q, 1, (1,), "S"), (turn_x, 1, 0, "V")),
             -1: (None, None, (turn_x, 1, 1, "V")),
         }
@@ -463,7 +463,7 @@ def tile_bayesianattention_pa_t_kernel(tc, x, wv_words, wv_scales, q, k, mask, s
             if ready is not None:
                 waiting.append((engine,) + ready)
 
-        first_plan = {0: (None, None, (turn_x, 1, 0, "V")), 1: (None, None, (turn_x, 1, 1, "S"))}
+        first_plan = {}
         first_project_plan = {0: 0, 2: 1}
         first_quantise_plan = {1: ((quantise_x, 1),), 3: ((quantise_v, 0), (mask_v, 0))}
 
@@ -503,9 +503,11 @@ def tile_bayesianattention_pa_t_kernel(tc, x, wv_words, wv_scales, q, k, mask, s
         mask_t = turn_mask()
         copy_out("V", *turn_x(0, 0))
         copy_out("V", *turn_x(0, 1))
-        prior_diagonal(0, mask_t)
-        copy_out("S", *turn_k(1, both))
+        copy_out("V", *turn_k(1, both))
         copy_out("S", *turn_q(1, both))
+        copy_out("S", *turn_x(1, 0))
+        prior_diagonal(0, mask_t)
+        copy_out("S", *turn_x(1, 1))
         prior_diagonal(1, mask_t)
         quantise_x(0)
 
@@ -517,9 +519,10 @@ def tile_bayesianattention_pa_t_kernel(tc, x, wv_words, wv_scales, q, k, mask, s
                 if n >= delay and (n - delay) % GROUPS == 0 and (n - delay) // GROUPS < B // TWIN:
                     invert_sums(kind, (n - delay) // GROUPS)
             if_group(score_tile, n, 0)
-            turn(n, 1)
+            quantise(n)
             if_group(multiply, n - 4)
             project(n)
+            turn(n, 1)
             turn(n, 2)
             empty(1)
             if 0 <= n - 1 < len(groups):
@@ -528,7 +531,6 @@ def tile_bayesianattention_pa_t_kernel(tc, x, wv_words, wv_scales, q, k, mask, s
             empty(len(waiting) - 1)
             if_group(exponential, n, 0)
             empty(len(waiting))
-            quantise(n)
             if_group(divide_and_store, n - 4)
 
         last = len(groups) - 1

@@ -480,12 +480,12 @@ def tile_bayesianattention_pa_t_kernel(tc, x, wv_words, wv_scales, q, k, mask, s
             for b, entry in planned(n, first_plan, plan):
                 if entry[place] is not None:
                     function, j, part, engine = entry[place]
-                    fill("V" if n < 1 else engine, function, b + j, part)
+                    fill("V" if n < 2 else engine, function, b + j, part)
 
         def project(n):
             for b, j in planned(n, first_project_plan, project_plan):
                 for h in range(H):
-                    fill("S", project_v, b + j, h)
+                    fill("V" if n == 0 and h == 0 else "S", project_v, b + j, h)
 
         def quantise(n):
             for b, entry in planned(n, first_quantise_plan, quantise_plan):

@@ -438,11 +438,11 @@ def tile_bayesianattention_pa_t_kernel(tc, x, wv_words, wv_scales, q, k, mask, s
         both = (0, 1)
         plan = {
             -6: ((turn_k, 0, (0,), "S"), (turn_k, 0, (1,), "S"), None),
-            -5: ((turn_q, 0, (0,), "S"), (turn_q, 0, (1,), "S"), None),
+            -5: ((turn_q, 0, (0,), "V"), (turn_q, 0, (1,), "V"), None),
             -4: (None, None, (turn_x, 0, 0, "V")),
-            -3: ((turn_k, 1, (0,), "S"), (turn_k, 1, (1,), "S"), (turn_x, 0, 1, "V")),
-            -2: ((turn_q, 1, (0,), "S"), (turn_q, 1, (1,), "S"), (turn_x, 1, 0, "V")),
-            -1: (None, None, (turn_x, 1, 1, "V")),
+            -3: ((turn_k, 1, (0,), "S"), (turn_k, 1, (1,), "S"), (turn_x, 0, 1, "S")),
+            -2: ((turn_q, 1, (0,), "V"), (turn_q, 1, (1,), "V"), (turn_x, 1, 0, "V")),
+            -1: (None, None, (turn_x, 1, 1, "S")),
         }
         project_plan = {-1: 0, 2: 1}
         quantise_plan = {

import math
from contextlib import ExitStack

import concourse.mybir as mybir
from concourse.masks import make_identity

F32 = mybir.dt.float32
BF16 = mybir.dt.bfloat16
I32 = mybir.dt.int32
U32 = mybir.dt.uint32
U8 = mybir.dt.uint8
FP8X4 = mybir.dt.float8_e4m3fn_x4
ALU = mybir.AluOpType
ACT = mybir.ActivationFunctionType
AX = mybir.AxisListType

B, S, D, H, HD = 8, 512, 512, 2, 128
E = H * HD
P = 128
HALF = P // 2
NT = S // P
PACK = 4
EPS = 1e-5
ROOT_HD = HD**0.5
TWIN = 2
RING = 4
GROUPS = 6

KEY_TILE = ((0, 2, 1, 3), (3, 0, 2, 1))

FLOPS = 2 * B * S * D * E + 2 * (2 * B * H * S * S * HD)


def tile_bayesianattention_pa_t_kernel(tc, x, wv_words, wv_scales, q, k, mask, shape, scale, loc, out):
    nc = tc.nc
    with ExitStack() as ctx:
        const = ctx.enter_context(tc.tile_pool(name="const", bufs=1))
        inputs = ctx.enter_context(tc.tile_pool(name="inputs", bufs=B))
        batch = ctx.enter_context(tc.tile_pool(name="batch", bufs=4))
        twins = ctx.enter_context(tc.tile_pool(name="twins", bufs=2))
        work = ctx.enter_context(tc.tile_pool(name="work", bufs=5))
        stats = ctx.enter_context(tc.tile_pool(name="stats", bufs=8))
        results = ctx.enter_context(tc.tile_pool(name="results", bufs=3))
        score_psum = ctx.enter_context(tc.psum_pool(name="score_psum", bufs=2))
        ring_psum = ctx.enter_context(tc.psum_pool(name="ring_psum", bufs=4))
        o_psum = ctx.enter_context(tc.psum_pool(name="o_psum", bufs=2))
        ctx.enter_context(tc.manual_schedule())

        w_scales = const.tile([P, E], U8, align_bytes=64)
        nc.vector.memset(w_scales[:].bitcast(I32), 0)
        params = const.tile([P, 3, 16], BF16)
        nc.vector.memset(params[:].rearrange("p v h -> p (v h)").bitcast(I32), 0)
        ones_bf = const.tile([P, P], BF16)
        nc.vector.memset(ones_bf[:], 1.0)
        for i, src in enumerate((loc, scale, shape)):
            nc.sync.dma_start(out=params[0:1, i, 0:H], in_=src.rearrange("a h b c -> (a b c) h"))

        q_sb, k_sb, x_sb = [], [], []

        def load_batch(b):
            k_sb.append(inputs.tile([P, NT, E], BF16, name="k_sb"))
            nc.sync.dma_start(out=k_sb[b][:], in_=k[b].rearrange("(t p) h d -> p t (h d)", p=P))
            q_sb.append(inputs.tile([P, NT, E], BF16, name="q_sb"))
            nc.sync.dma_start(out=q_sb[b][:], in_=q[b].rearrange("(t p) h d -> p t (h d)", p=P))
            x_sb.append(inputs.tile([P, PACK, D], BF16, name="x_sb"))
            nc.sync.dma_start(
                out=x_sb[b][:].rearrange("p (u e) c -> p u (e c)", u=2),
                in_=x[b].rearrange("(u p e) c -> p u (e c)", u=2, e=2),
            )

        load_batch(0)
        mask_sb = const.tile([P, NT, P], BF16)
        for t in range(NT):
            nc.sync.dma_start(out=mask_sb[:, t, :], in_=mask[0, 0, t * P : (t + 1) * P, t * P : (t + 1) * P])

        load_batch(1)
        w_codes = const.tile([P, E], U32, align_bytes=64)
        nc.sync.dma_start(out=w_codes[:].bitcast(I32), in_=wv_words[0].rearrange("p n t -> p (n t)").bitcast(I32))
        for quad in range(4):
            nc.sync.dma_start(
                out=w_scales[32 * quad : 32 * quad + 4, :].bitcast(I32),
                in_=wv_scales[0, 4 * quad : 4 * quad + 4, :].bitcast(I32),
            )
        for b in range(2, B):
            load_batch(b)

        eps_col = const.tile([P, 1], F32)
        nc.vector.memset(eps_col[:], EPS)
        warm = const.tile([P, 1], F32)
        nc.scalar.activation(out=warm[:], in_=eps_col[:], func=ACT.Exp)
        log_root = const.tile([P, 1], F32)
        nc.vector.tensor_scalar(
            out=log_root[:], in0=eps_col[:], scalar1=0.0, scalar2=math.log(ROOT_HD), op0=ALU.mult, op1=ALU.add
        )
        ident_f32 = const.tile([P, P], F32)
        make_identity(nc, ident_f32[:])
        ident_bf = const.tile([P, P], BF16)
        nc.vector.tensor_copy(out=ident_bf[:], in_=ident_f32[:])
        minus_ident_bf = const.tile([P, P], BF16)
        nc.vector.tensor_scalar(
            out=minus_ident_bf[:], in0=ident_f32[:], scalar1=-1.0, scalar2=None, op0=ALU.mult
        )
        swapped_f32 = const.tile([P, P], F32)
        nc.vector.tensor_copy(out=swapped_f32[:, :HALF], in_=ident_f32[:, HALF:])
        nc.vector.tensor_copy(out=swapped_f32[:, HALF:], in_=ident_f32[:, :HALF])
        dist = const.tile([P, S], F32)
        nc.gpsimd.iota(dist[:], pattern=[[-1, S]], base=0, channel_multiplier=1, allow_small_or_imprecise_dtypes=True)

        e_long, e_short = {}, []
        for h in range(H):
            for j in range(TWIN):
                e_long[j, h] = const.tile([P, 2, NT, P], BF16, name="e_long%d%d" % (j, h))
                dead = KEY_TILE[j].index(NT - 1)
                nc.gpsimd.memset(e_long[j, h][:, 0, dead, :].bitcast(I32), 0)
            e_short.append(const.tile([P, 2, NT, P], BF16, name="e_short%d" % h))
            nc.gpsimd.memset(e_short[h][:, 0, 2:NT, :].rearrange("p t c -> p (t c)").bitcast(I32), 0)
        v_masked = [const.tile([P, H, TWIN, HD], U32, name="v_masked%d" % i, align_bytes=64) for i in range(2)]
        for i in range(2):
            nc.gpsimd.memset(v_masked[i][:].rearrange("p h j d -> p (h j d)").bitcast(I32), 0)

        slope = const.tile([P, H], F32)
        exp_loc = const.tile([P, H], F32)
        exp_neg_loc = const.tile([P, H], F32)
        shape_f = const.tile([P, H], F32)
        offset = const.tile([P, H], F32)
        z = const.tile([P, H, S], F32)
        abs_z = const.tile([P, H, S], F32)
        log_z = const.tile([P, H, S], F32)
        prior_t = const.tile([P, H, S], F32)
        diag_t = const.tile([P, H, NT, P], F32)

        def ring_bank(tile_shape, dtype):
            return ring_psum.tile(tile_shape, dtype, tag="bank", name="ring_bank")

        def prior_distance():
            spread = score_psum.tile([P, 3, H], F32, tag="bank", name="spread")
            nc.tensor.matmul(out=spread[:], lhsT=ones_bf[:], rhs=params[:, :, 0:H], start=True, stop=True)
            nc.scalar.activation(out=exp_loc[:], in_=spread[:, 0, :], func=ACT.Exp)
            nc.scalar.activation(out=exp_neg_loc[:], in_=spread[:, 0, :], func=ACT.Exp, scale=-1.0)
            nc.scalar.activation(out=slope[:], in_=spread[:, 1, :], func=ACT.Exp)
            nc.scalar.activation(out=warm[:], in_=slope[:, 0:1], func=ACT.Ln)
            nc.vector.tensor_sub(out=offset[:], in0=exp_loc[:], in1=exp_neg_loc[:])
            for h in range(H):
                nc.vector.tensor_scalar(
                    out=z[:, h, :], in0=dist[:], scalar1=offset[:, h : h + 1], scalar2=slope[:, h : h + 1],
                    op0=ALU.subtract, op1=ALU.mult,
                )
            for h in range(H):
                nc.vector.scalar_tensor_tensor(
                    out=abs_z[:, h, :], in0=z[:, h, :], scalar=-1.0, in1=z[:, h, :], op0=ALU.mult, op1=ALU.max
                )
            nc.vector.tensor_copy(out=shape_f[:], in_=spread[:, 2, :])

        def prior_power():
            for h in range(H):
                nc.scalar.activation(out=log_z[:, h, :], in_=abs_z[:, h, :], func=ACT.Ln, bias=eps_col[:])
            for h in range(H):
                nc.scalar.activation(
                    out=prior_t[:, h, :], in_=log_z[:, h, :], func=ACT.Exp, scale=shape_f[:, h : h + 1],
                    bias=log_root[:],
                )

        def turn_mask():
            bank = score_psum.tile([P, NT, P], BF16, tag="bank", name="mask_bank")
            for t in range(NT):
                nc.tensor.transpose(bank[:, t, :], mask_sb[:, t, :], ident_bf[:])
            return bank

        def prior_diagonal(h, mask_t):
            nc.vector.scalar_tensor_tensor(
                out=diag_t[:, h, :, :], in0=mask_t[:], scalar=-ROOT_HD,
                in1=prior_t[:, h, :P].unsqueeze(1).to_broadcast([P, NT, P]), op0=ALU.mult, op1=ALU.add,
            )

        x_grouped, x_codes, x_scales, v_grouped = {}, {}, {}, {}
        q_t, k_t, v_codes, v_scales = {}, {}, {}, {}

        def copy_out(engine, dst, src):
            if engine == "V":
                nc.vector.tensor_copy(out=dst, in_=src)
            else:
                nc.scalar.copy(out=dst, in_=src)

        def turn_rows(rows, turned, tiles, identity, heads):
            if 0 in heads:
                half_full.append(ring_bank([P, H, NT, P], BF16))
            bank = half_full[0]
            for h in heads:
                for pos in range(NT):
                    nc.tensor.matmul(
                        out=bank[:, h, pos, :], lhsT=rows[:, tiles[pos], h * HD : (h + 1) * HD], rhs=identity[:],
                        start=True, stop=True,
                    )
            if H - 1 not in heads:
                return None
            half_full.clear()
            return turned[:], bank[:]

        half_full = []

        def turn_k(b, heads):
            if 0 in heads:
                k_t[b] = batch.tile([P, H, NT, P], BF16, name="k_t")
            return turn_rows(k_sb[b], k_t[b], KEY_TILE[b % TWIN], ident_bf, heads)

        def turn_q(b, heads):
            if 0 in heads:
                q_t[b] = batch.tile([P, H, NT, P], BF16, name="q_t")
            return turn_rows(q_sb[b], q_t[b], range(NT), minus_ident_bf, heads)

        def turn_x(b, e):
            if e == 0:
                x_grouped[b] = batch.tile([P, PACK, P, PACK], BF16, name="x_grouped", align_bytes=64)
            x_words = x_sb[b][:].bitcast(F32)
            grouped_words = (
                x_grouped[b][:].rearrange("p t r c -> p (t r c)").bitcast(F32).rearrange("p (t r f) -> p t r f", t=PACK, f=2)
            )
            bank = ring_bank([P, 2, 2, 2, HALF], F32)
            for u in range(2):
                place = KEY_TILE[b % TWIN].index(2 * u)
                identity = ident_f32 if place < 2 else swapped_f32
                for f in range(2):
                    nc.tensor.matmul(
                        out=bank[:, :, f, place % 2, :], lhsT=x_words[:, 2 * u + e, f : D // 2 : 2],
                        rhs=identity[:].rearrange("p (v r) -> p v r", v=2), is_transpose=True, start=True, stop=True,
                    )
            return grouped_words[:, e : PACK : 2, :, :], bank[:].rearrange("p v f h r -> p v (h r) f")

        def quantise_x(b):
            x_codes[b] = batch.tile([P, PACK * P], U32, name="x_codes", align_bytes=64)
            x_scales[b] = batch.tile([P, PACK * P], U8, name="x_scales", align_bytes=64)
            nc.vector.quantize_mx(
                out=x_codes[b][:].bitcast(FP8X4), scales=x_scales[b][:],
                in_=x_grouped[b][:].rearrange("p t r c -> p (t r c)"),
            )

        def project_v(b, h):
            twin, j = divmod(b, TWIN)
            if h == 0 and j == 0:
                v_grouped[twin] = twins.tile([P, H, TWIN, HD, PACK], BF16, name="v_grouped", align_bytes=64)
            bank = ring_bank([P, PACK, HD], F32)
            for t in range(PACK):
                nc.tensor.matmul_mx(
                    out=bank[:, t, :],
                    lhsT=x_codes[b][:, t * P : (t + 1) * P].bitcast(FP8X4),
                    lhsT_scale=x_scales[b][:, t * P : (t + 1) * P],
                    rhs=w_codes[:, h * HD : (h + 1) * HD].bitcast(FP8X4),
                    rhs_scale=w_scales[:, h * HD : (h + 1) * HD],
                    start=True,
                    stop=True,
                )
            return v_grouped[twin][:, h, j, :, :], bank[:].rearrange("p t d -> p d t")

        def quantise_v(b):
            twin = b // TWIN
            v_codes[twin] = twins.tile([P, H, TWIN, HD], U32, name="v_codes", align_bytes=64)
            v_scales[twin] = twins.tile([P, H, TWIN, HD], U8, name="v_scales", align_bytes=64)
            nc.vector.quantize_mx(
                out=v_codes[twin][:].rearrange("p h j d -> p (h j d)").bitcast(FP8X4),
                scales=v_scales[twin][:].rearrange("p h j d -> p (h j d)"),
                in_=v_grouped[twin][:].rearrange("p h j d t -> p (h j d t)"),
            )

        def mask_v(b):
            twin = b // TWIN
            for j in range(TWIN):
                half = slice(j * HALF, (j + 1) * HALF)
                nc.sync.dma_start(
                    out=v_masked[twin % 2][half, :, j, :].bitcast(I32), in_=v_codes[twin][half, :, j, :].bitcast(I32)
                )

        groups = []
        for twin in range(B // TWIN):
            groups += [("long", twin, j, h) for j in range(TWIN) for h in range(H)]
            groups += [("short", twin, None, h) for h in range(H)]
        row_sum, inv_sum, e_grouped, e_codes, e_scales, o_bank, o_short = {}, {}, {}, {}, {}, {}, {}

        def score_bank():
            return score_psum.tile([P, NT, P], F32, tag="bank", name="score_bank")

        def add_scores(bank, b, h, it, positions, columns):
            for i, pos in enumerate(positions):
                jt = KEY_TILE[b % TWIN][pos]
                nc.tensor.matmul(
                    out=bank[:, pos, :] if columns is None else bank[:, columns, :],
                    lhsT=diag_t[:, h, it, :] if jt == it else prior_t[:, h, (it - jt) * P : (it - jt + 1) * P],
                    rhs=ident_f32[:],
                    is_transpose=True,
                    start=(i == 0),
                    stop=False,
                )
            step = positions[1] - positions[0] if len(positions) > 1 else 1
            span = slice(positions[0], positions[-1] + 1, step)
            nc.tensor.matmul(
                out=bank[:, span, :] if columns is None else bank[:, columns, :],
                lhsT=q_t[b][:, h, it, :], rhs=k_t[b][:, h, span, :], start=False, stop=True,
            )

        def negate(neg, bank_view, low):
            nc.vector.tensor_scalar(
                out=neg, in0=bank_view, scalar1=1.0 / ROOT_HD, scalar2=None, op0=ALU.mult, op1=ALU.min, accum_out=low
            )

        def exponential(n, ii):
            for dst, src, bias, total in pending[n, ii]:
                nc.scalar.activation(out=dst, in_=src, func=ACT.Exp, scale=-1.0, bias=bias, accum_out=total)

        pending = {}

        def long_tile(n, ii):
            kind, twin, j, h = groups[n]
            b = TWIN * twin + j
            if h == 0 and j == 0 and ii == 1:
                row_sum["long", twin] = stats.tile([P, TWIN, 2, H], F32, name="row_sum")
            it = 2 + ii
            live = [pos for pos in range(NT) if KEY_TILE[j][pos] <= it]
            span = slice(live[0], live[-1] + 1)
            bank = score_bank()
            add_scores(bank, b, h, it, live, None)
            neg_s = work.tile([P, NT, P], F32, name="neg_s")
            low = stats.tile([P, TWIN], F32, name="low")
            negate(neg_s[:, span, :], bank[:, span, :], low[:, 0:1])
            pending[n, ii] = [
                (e_long[j, h][:, ii, span, :], neg_s[:, span, :], low[:, 0:1], row_sum[kind, twin][:, j, ii, h : h + 1])
            ]

        def short_tile(n, it):
            kind, twin, j, h = groups[n]
            if it == 1 and h == 0:
                row_sum["short", twin] = stats.tile([P, H, 2, TWIN], F32, name="row_sum")
            bank = score_bank()
            for j in range(TWIN):
                b = TWIN * twin + j
                add_scores(bank, b, h, it, [pos for pos in range(NT) if KEY_TILE[j][pos] <= it], None)
            neg_s = work.tile([P, NT, P], F32, name="neg_s")
            low = stats.tile([P, TWIN], F32, name="low")
            pending[n, it] = []
            for j in range(TWIN):
                span = slice(j, NT, TWIN) if it == 1 else slice(j, j + 1)
                negate(neg_s[:, span, :], bank[:, span, :], low[:, j : j + 1])
                pending[n, it].append(
                    (e_short[h][:, it, span, :], neg_s[:, span, :], low[:, j : j + 1], row_sum[kind, twin][:, h, it, j : j + 1])
                )

        def score_tile(n, ii):
            if groups[n][0] == "long":
                long_tile(n, ii)
            else:
                short_tile(n, ii)

        def turn_e(n, first=0, count=2):
            kind, twin, j, h = groups[n]
            rows = e_long[j, h] if kind == "long" else e_short[h]
            bank = ring_bank([P, count, 2, P], F32)
            for i in range(count):
                words = rows[:, first + i, :, :].rearrange("p t c -> p (t c)").bitcast(F32)
                for u in range(2):
                    nc.tensor.transpose(bank[:, i, u, :], words[:, u * P : (u + 1) * P], ident_f32[:])
            if n not in e_grouped:
                e_grouped[n] = work.tile([P, 2, P, PACK], BF16, name="e_grouped", align_bytes=64)
            grouped_words = (
                e_grouped[n][:].rearrange("p t i c -> p (t i c)").bitcast(F32).rearrange("p (t i u) -> p t i u", t=2, u=2)
            )
            return grouped_words[:, first : first + count, :, :], bank[:].rearrange("p t u i -> p t i u")

        def quantise_e(n, first=0, count=2):
            if n not in e_codes:
                e_codes[n] = work.tile([P, 2, P], U32, name="e_codes", align_bytes=64)
                e_scales[n] = work.tile([P, 2, P], U8, name="e_scales", align_bytes=64)
            tiles = slice(first, first + count)
            nc.vector.quantize_mx(
                out=e_codes[n][:, tiles, :].rearrange("p t i -> p (t i)").bitcast(FP8X4),
                scales=e_scales[n][:, tiles, :].rearrange("p t i -> p (t i)"),
                in_=e_grouped[n][:, tiles, :, :].rearrange("p t i c -> p (t i c)"),
            )

        def multiply(n, first=0, count=2):
            kind, twin, j, h = groups[n]
            if kind == "short":
                if n not in o_bank:
                    pool = o_psum if n < len(groups) - 1 else score_psum
                    o_bank[n] = pool.tile([P, 2, TWIN, HD], F32, tag="bank", name="o_bank")
                codes = v_masked[twin % 2][:, h, :, :].rearrange("p j d -> p (j d)")
                scales = v_scales[twin][:, h, :, :].rearrange("p j d -> p (j d)")
            else:
                o_bank[n] = o_psum.tile([P, 2, H, HD], F32, tag="bank", name="o_bank") if h == 0 else o_bank[n - 1]
                codes = v_codes[twin][:, h, j, :]
                scales = v_scales[twin][:, h, j, :]
            for ii in range(first, first + count):
                nc.tensor.matmul_mx(
                    out=o_bank[n][:, ii, :, :].rearrange("p a d -> p (a d)") if kind == "short" else o_bank[n][:, ii, h, :],
                    lhsT=e_codes[n][:, ii, :].bitcast(FP8X4),
                    lhsT_scale=e_scales[n][:, ii, :],
                    rhs=codes.bitcast(FP8X4),
                    rhs_scale=scales,
                    start=True,
                    stop=True,
                )

        def invert_sums(kind, twin):
            inv_sum[kind, twin] = stats.tile([P, 2, 2, 2], F32, name="inv_sum")
            nc.vector.reciprocal(out=inv_sum[kind, twin][:], in_=row_sum[kind, twin][:])

        def divide_and_store(n, first=0, count=2):
            kind, twin, j, h = groups[n]
            if kind == "long" and h == 0:
                return
            factor = inv_sum[kind, twin][:, j if kind == "long" else h, :, :].unsqueeze(3).to_broadcast([P, 2, 2, HD])
            if kind == "long":
                o_sb = results.tile([P, 2, H, HD], F32, name="o_sb")
                if n < len(groups) - GROUPS // 2:
                    nc.vector.tensor_tensor(out=o_sb[:], in0=o_bank[n][:], in1=factor, op=ALU.mult)
                else:
                    for ii in range(2):
                        for head in range(H):
                            nc.scalar.activation(
                                out=o_sb[:, ii, head, :], in_=o_bank[n][:, ii, head, :], func=ACT.Copy,
                                scale=inv_sum[kind, twin][:, j, ii, head : head + 1],
                            )
                nc.sync.dma_start(
                    out=out[TWIN * twin + j, 2 * P : 4 * P, :].rearrange("(t p) n -> p t n", p=P),
                    in_=o_sb[:].rearrange("p t h d -> p t (h d)"),
                )
                return
            if h == 0:
                o_short[twin] = results.tile([P, 2, TWIN, H, HD], F32, name="o_short")
            tiles = slice(first, first + count)
            nc.vector.tensor_tensor(
                out=o_short[twin][:, tiles, :, h, :], in0=o_bank[n][:, tiles, :, :], in1=factor[:, tiles, :, :], op=ALU.mult
            )
            if h == H - 1:
                for jj in range(TWIN):
                    nc.sync.dma_start(
                        out=out[TWIN * twin + jj, first * P : (first + count) * P, :].rearrange("(t p) n -> p t n", p=P),
                        in_=o_short[twin][:, tiles, jj, :, :].rearrange("p t h d -> p t (h d)"),
                    )

        both = (0, 1)
        plan = {
            -6: ((turn_k, 0, (0,), "S"), (turn_k, 0, (1,), "S"), None),
            -5: ((turn_q, 0, (0,), "V"), (turn_q, 0, (1,), "V"), None),
            -4: (None, None, (turn_x, 0, 0, "V")),
            -3: ((turn_k, 1, (0,), "S"), (turn_k, 1, (1,), "S"), (turn_x, 0, 1, "S")),
            -2: ((turn_q, 1, (0,), "V"), (turn_q, 1, (1,), "V"), (turn_x, 1, 0, "V")),
            -1: (None, None, (turn_x, 1, 1, "S")),
        }
        project_plan = {-1: 0, 2: 1}
        quantise_plan = {
            -2: ((quantise_x, 0),), 0: ((quantise_x, 1),), 3: ((quantise_v, 0), (mask_v, 0)),
        }

        waiting = []

        def empty(count):
            for ready in waiting[:count]:
                copy_out(*ready)
            waiting[:count] = []

        def fill(engine, function, *args):
            if len(waiting) + len(half_full) == RING:
                empty(1)
            ready = function(*args)
            if ready is not None:
                waiting.append((engine,) + ready)

        first_plan = {}
        first_project_plan = {0: 0, 2: 1}
        first_quantise_plan = {1: ((quantise_x, 1),), 3: ((quantise_v, 0), (mask_v, 0))}

        def planned(n, plan_of_first, plan_of_others):
            found = []
            for twin in range(B // TWIN):
                step = n - GROUPS * twin
                entry = (plan_of_others if twin else plan_of_first).get(step)
                if entry is not None:
                    found.append((TWIN * twin, entry))
            return found

        def turn(n, place):
            for b, entry in planned(n, first_plan, plan):
                if entry[place] is not None:
                    function, j, part, engine = entry[place]
                    fill("V" if n < 2 else engine, function, b + j, part)

        def project(n):
            for b, j in planned(n, first_project_plan, project_plan):
                for h in range(H):
                    fill("V" if n == 0 and h == 0 else "S", project_v, b + j, h)

        def quantise(n):
            for b, entry in planned(n, first_quantise_plan, quantise_plan):
                for function, j, *rest in entry:
                    function(b + j, *rest)

        def if_group(step, n, *args):
            if 0 <= n < len(groups):
                step(n, *args)

        prior_distance()
        prior_power()
        copy_out("V", *turn_k(0, both))
        copy_out("V", *turn_q(0, both))
        mask_t = turn_mask()
        copy_out("V", *turn_x(0, 0))
        copy_out("V", *turn_x(0, 1))
        copy_out("V", *turn_k(1, both))
        copy_out("S", *turn_q(1, both))
        copy_out("S", *turn_x(1, 0))
        prior_diagonal(0, mask_t)
        copy_out("S", *turn_x(1, 1))
        prior_diagonal(1, mask_t)
        quantise_x(0)

        for n in range(len(groups)):
            if_group(score_tile, n, 1)
            turn(n, 0)
            if_group(quantise_e, n - 3)
            for kind, delay in (("long", 5), ("short", 8)):
                if n >= delay and (n - delay) % GROUPS == 0 and (n - delay) // GROUPS < B // TWIN:
                    invert_sums(kind, (n - delay) // GROUPS)
            if_group(score_tile, n, 0)
            quantise(n)
            if_group(multiply, n - 4)
            project(n)
            turn(n, 1)
            turn(n, 2)
            empty(1)
            if 0 <= n - 1 < len(groups):
                fill("S", turn_e, n - 1)
            if_group(exponential, n, 1)
            empty(len(waiting) - 1)
            if_group(exponential, n, 0)
            empty(len(waiting))
            if_group(divide_and_store, n - 4)

        last = len(groups) - 1
        multiply(last - 3)
        fill("S", turn_e, last, 1, 1)
        fill("S", turn_e, last, 0, 1)
        quantise_e(last - 2)
        multiply(last - 2)
        quantise_e(last - 1)
        invert_sums("short", B // TWIN - 1)
        empty(2)
        quantise_e(last, 1, 1)
        multiply(last - 1)
        divide_and_store(last - 2)
        quantise_e(last, 0, 1)
        multiply(last, 1, 1)
        divide_and_store(last - 1)
        multiply(last, 0, 1)
        divide_and_store(last, 1, 1)
        divide_and_store(last, 0, 1)
